import numpy as np
import ml_dtypes


def mxq(x, axis, fmt="e4m3"):
    dtype, down = {"e4m3": (ml_dtypes.float8_e4m3fn, 7), "e5m2": (ml_dtypes.float8_e5m2, 14)}[fmt]
    v = np.moveaxis(np.asarray(x, np.float32).astype(ml_dtypes.bfloat16).astype(np.float64), axis, -1)
    blocks = v.reshape(v.shape[:-1] + (-1, 32))
    amax = np.abs(blocks).max(-1, keepdims=True)
    byte = np.maximum(np.where(amax > 0, np.frexp(amax)[1] - 1 + 127, 0) - down, 1)
    scale = np.exp2(byte - 127.0)
    codes = (blocks / scale).astype(np.float32).astype(dtype).astype(np.float64)
    return np.moveaxis((codes * scale).reshape(v.shape), -1, axis)


WIDE = False


def mx_kscale(k):
    if not WIDE:
        return np.ones(k)
    levels = np.array([10, -10, 5, -5, 0])
    a = np.random.permutation(np.resize(levels, k // 512 * 4)).reshape(k // 512, 4)
    idx = np.arange(k)
    return np.exp2(a[idx // 512, idx % 128 // 32])


BF16 = ml_dtypes.bfloat16


def bf(x):
    return np.asarray(x, np.float32).astype(BF16)


def f64(x):
    return np.asarray(x).astype(np.float64)


B, CL, CH, CK, CV, CO, H, W = 2, 1024, 2048, 256, 512, 1024, 24, 24
N = H * W
PSP = (1, 3, 6, 8)
EPS = 1e-5


def psp(x):
    b, c, h, w = x.shape
    return np.concatenate(
        [x.reshape(b, c, s, h // s, s, w // s).mean(axis=(3, 5)).reshape(b, c, s * s) for s in PSP], axis=2)


def setup_inputs():
    s = mx_kscale(CL)
    return {"low_feats": bf(np.random.standard_normal((B, CL, H, W)) * s[None, :, None, None]),
            "wk": bf(np.random.standard_normal((CK, CL)) * 2.5 / np.sqrt(CL) / s[None, :]),
            "bk": bf(np.random.standard_normal(CK) * 0.3),
            "gk": bf(np.random.uniform(0.5, 1.5, CK)),
            "bek": bf(np.random.standard_normal(CK) * 0.3),
            "mk": bf(np.random.standard_normal(CK) * 0.3),
            "vk": bf(np.random.uniform(0.5, 1.5, CK)),
            "wv": bf(np.random.standard_normal((CV, CL)) * 3.0 / np.sqrt(CL) / s[None, :]),
            "bv": bf(np.random.standard_normal(CV) * 0.3)}


def reference(low_feats, wk, bk, gk, bek, mk, vk, wv, bv):
    xq = mxq(f64(low_feats).reshape(B, CL, N), 1, "e4m3")
    v = (mxq(f64(wv), 1, "e4m3") @ xq) + f64(bv)[None, :, None]
    value = psp(v.reshape(B, CV, H, W)).transpose(0, 2, 1)
    u = (mxq(f64(wk), 1, "e4m3") @ xq) + f64(bk)[None, :, None]
    sc = f64(gk) / np.sqrt(f64(vk) + EPS)
    r = np.maximum((u - f64(mk)[None, :, None]) * sc[None, :, None] + f64(bek)[None, :, None], 0.0)
    key = psp(r.reshape(B, CK, H, W))
    return value, key

@@ -1,0 +1,380 @@
+from contextlib import ExitStack
+
+import concourse.mybir as mybir
+from concourse.masks import make_identity
+
+F32 = mybir.dt.float32
+BF16 = mybir.dt.bfloat16
+U32 = mybir.dt.uint32
+U8 = mybir.dt.uint8
+FP8X4 = mybir.dt.float8_e4m3fn_x4
+ALU = mybir.AluOpType
+ACT = mybir.ActivationFunctionType
+AX = mybir.AxisListType
+
+P = 128
+NB = 2
+NPX = 576
+NX = NB * NPX
+CH = 768
+NLOC = 110
+EPS = 1e-5
+FLOPS = 2 * 768 * 1024 * 1152
+PX_STARTS = (0, 128, 256, 384, 448)
+
+
+def tile_afnb_pa_kernel(tc, low_feats, wk, bk, gk, bek, mk, vk, wv, bv, out_0, out_1):
+    nc = tc.nc
+    with ExitStack() as ctx:
+        keep = ctx.enter_context(tc.tile_pool(name="keep", bufs=1))
+        work = ctx.enter_context(tc.tile_pool(name="work", bufs=2))
+        vpool = ctx.enter_context(tc.tile_pool(name="vpool", bufs=3))
+        ps_a = ctx.enter_context(tc.psum_pool(name="ps_a", bufs=2))
+        ps_x = ctx.enter_context(tc.psum_pool(name="ps_x", bufs=2))
+        ps_b = ctx.enter_context(tc.psum_pool(name="ps_b", bufs=2))
+        ps_t = ctx.enter_context(tc.psum_pool(name="ps_t", bufs=2))
+
+        prm = keep.tile([P, P], BF16)
+        nc.vector.memset(prm[:], 0.0)
+        bvrow = keep.tile([P, 512], BF16)
+        nc.vector.memset(bvrow[:], 0.0)
+        for i, vec in enumerate((bk, gk, bek, mk, vk)):
+            nc.scalar.dma_start(
+                out=prm[2 * i : 2 * i + 2, :], in_=vec.rearrange("(r p) -> r p", p=P)
+            )
+        nc.scalar.dma_start(out=bvrow[0:1, :], in_=bv.rearrange("(o c) -> o c", o=1))
+
+        w_sb = keep.tile([P, 6 * 1024], BF16)
+        xr = []
+        for b in range(NB):
+            row = []
+            for g in range(2):
+                xr_bg = keep.tile([P, 4, NPX], BF16, name="xr%d%d" % (b, g))
+                row.append(xr_bg)
+            xr.append(row)
+
+        def load_x(b, g):
+            nc.sync.dma_start(
+                out=xr[b][g][:].rearrange("p (u e) n -> p u e n", e=2),
+                in_=low_feats[b, 512 * g : 512 * g + 512].rearrange(
+                    "(u q e) h w -> q u e (h w)", u=2, e=2
+                ),
+            )
+
+        def load_w(r0, rows):
+            nc.sync.dma_start(
+                out=w_sb[:, 1024 * r0 : 1024 * (r0 + 2)].rearrange("p (r k) -> p r k", k=1024),
+                in_=rows.rearrange("(r p) k -> p r k", p=P),
+            )
+
+        load_w(2, wv[256:512, :])
+        load_x(0, 0)
+        load_x(0, 1)
+        load_w(0, wv[0:256, :])
+        load_w(4, wk)
+        load_x(1, 0)
+        load_x(1, 1)
+
+        ident_b = keep.tile([P, P], BF16)
+        make_identity(nc, ident_b[:])
+        ident_f = keep.tile([P, P], F32)
+        make_identity(nc, ident_f[:])
+
+        warm = keep.tile([P, 1], F32)
+        nc.vector.memset(warm[:], 1.0)
+        nc.scalar.activation(out=warm[:], in_=warm[:], func=ACT.Sqrt)
+
+        q8 = keep.tile([P, 8, 24], BF16)
+        q6 = keep.tile([P, 6, 24], BF16)
+        q3 = keep.tile([P, 3, 24], BF16)
+        for qt, off, grid, bs in ((q8, 46, 8, 3), (q6, 10, 6, 4), (q3, 1, 3, 8)):
+            nc.vector.tensor_copy(
+                out=qt[:].rearrange("p g (c j) -> p g c j", j=bs),
+                in_=ident_b[:, off : off + grid * grid]
+                .rearrange("p (g c) -> p g c", c=grid)
+                .unsqueeze(3)
+                .to_broadcast([P, grid, grid, bs]),
+            )
+        member = keep.tile([P, 24, 24], BF16)
+        nc.vector.tensor_copy(
+            out=member[:].rearrange("p (g i) w -> p g i w", i=3),
+            in_=q8[:].unsqueeze(2).to_broadcast([P, 8, 3, 24]),
+        )
+        for qt, grid, bs in ((q6, 6, 4), (q3, 3, 8)):
+            mv = member[:].rearrange("p (g i) w -> p g i w", i=bs)
+            nc.vector.tensor_tensor(
+                out=mv, in0=mv, in1=qt[:].unsqueeze(2).to_broadcast([P, grid, bs, 24]), op=ALU.add
+            )
+        mflat = member[:].rearrange("p h w -> p (h w)")
+        nc.vector.tensor_scalar_add(out=mflat, in0=mflat, scalar1=ident_f[:, 0:1])
+        mtail = keep.tile([P, P], BF16)
+        nc.vector.memset(mtail[:], 0.0)
+        nc.vector.tensor_copy(out=mtail[:, 64:128], in_=mflat[:, 512:576])
+        pmem = ps_t.tile([P, 5, P], BF16, tag="T")
+        for m in range(4):
+            nc.tensor.transpose(
+                out=pmem[:, m, :], in_=mflat[:, P * m : P * m + P], identity=ident_b[:]
+            )
+        nc.tensor.transpose(out=pmem[:, 4, :], in_=mtail[:], identity=ident_b[:])
+        pmat = keep.tile([P, 5, P], F32)
+        nc.scalar.copy(out=pmat[:], in_=pmem[:])
+
+        ones = keep.tile([P, P], BF16)
+        nc.vector.memset(ones[:], 1.0)
+        wloc = keep.tile([P, NLOC], F32)
+        nc.vector.memset(wloc[:, 0:1], 576.0)
+        nc.vector.memset(wloc[:, 1:10], 64.0)
+        nc.vector.memset(wloc[:, 10:46], 16.0)
+        nc.vector.memset(wloc[:, 46:110], 9.0)
+        nc.vector.reciprocal(out=wloc[:], in_=wloc[:])
+        rtmp = keep.tile([P, NLOC], F32)
+        nc.vector.tensor_mul(out=rtmp[:], in0=ident_f[:, 0:NLOC], in1=wloc[:])
+        rs = keep.tile([P, 1], F32)
+        nc.vector.tensor_reduce(out=rs[:], in_=rtmp[:], axis=AX.X, op=ALU.add)
+        sums = keep.tile([P, NB, 4, P], F32)
+        nc.vector.memset(sums[:, :, :, NLOC:P], 0.0)
+
+        wf = w_sb[:].bitcast(F32)
+        wg = keep.tile([P, 2 * CH * 4], BF16, align_bytes=64)
+        wgf = wg[:].bitcast(F32).rearrange("p (g c u) -> p g c u", g=2, u=2)
+        wc = keep.tile([P, 2 * CH], U32, align_bytes=64)
+        wsc = keep.tile([P, 2 * CH], U8, align_bytes=64)
+
+        def weight_block(r, on_vector):
+            pw = ps_t.tile([P, 2, 2, P], F32, tag="T")
+            for g in range(2):
+                for u in range(2):
+                    c0 = 512 * r + 256 * g + 128 * u
+                    nc.tensor.transpose(
+                        out=pw[:, g, u, :], in_=wf[:, c0 : c0 + P], identity=ident_f[:]
+                    )
+            dst = wgf[:, :, P * r : P * r + P, :]
+            src = pw[:].rearrange("p g u c -> p g c u")
+            if on_vector:
+                nc.vector.tensor_copy(out=dst, in_=src)
+            else:
+                nc.scalar.copy(out=dst, in_=src)
+
+        def weight_quant(c0, c1):
+            for g in range(2):
+                lo = g * CH + c0
+                hi = g * CH + c1
+                nc.vector.quantize_mx(
+                    out=wc[:, lo:hi].bitcast(FP8X4),
+                    scales=wsc[:, lo:hi],
+                    in_=wg[:, 4 * lo : 4 * hi],
+                )
+
+        xg = keep.tile([P, 2 * NX * 4], BF16, align_bytes=64)
+        xc = keep.tile([P, 2 * NX], U32, align_bytes=64)
+        xs = keep.tile([P, 2 * NX], U8, align_bytes=64)
+
+        def regroup(b, g, a0, a1, on_vector):
+            base = g * NX + NPX * b
+            dst = xg[:, 4 * (base + a0) : 4 * (base + a1)].rearrange(
+                "p (c i t) -> p c t i", i=4, t=4
+            )
+            src = xr[b][g][:, :, a0:a1].rearrange("p t (c i) -> p c t i", i=4)
+            if on_vector:
+                nc.vector.tensor_copy(out=dst, in_=src)
+            else:
+                nc.scalar.copy(out=dst, in_=src)
+
+        def quant_x(g, lo, hi):
+            lo = g * NX + lo
+            hi = g * NX + hi
+            nc.vector.quantize_mx(
+                out=xc[:, lo:hi].bitcast(FP8X4),
+                scales=xs[:, lo:hi],
+                in_=xg[:, 4 * lo : 4 * hi],
+            )
+
+        weight_block(2, False)
+        weight_block(3, True)
+        regroup(0, 0, 0, 384, True)
+        regroup(0, 0, 384, 576, False)
+        weight_quant(256, 512)
+        quant_x(0, 0, 512)
+        quant_x(0, 512, 576)
+        regroup(0, 1, 0, 384, True)
+        regroup(0, 1, 384, 576, False)
+        quant_x(1, 0, 512)
+        quant_x(1, 512, 576)
+
+        def mx_group(out, blk, lo, n):
+            for g in range(2):
+                w0 = g * CH + P * blk
+                x0 = g * NX + lo
+                nc.tensor.matmul_mx(
+                    out=out,
+                    lhsT=wc[:, w0 : w0 + P].bitcast(FP8X4),
+                    lhsT_scale=wsc[:, w0 : w0 + P],
+                    rhs=xc[:, x0 : x0 + n].bitcast(FP8X4),
+                    rhs_scale=xs[:, x0 : x0 + n],
+                    start=(g == 0),
+                    stop=(g == 1),
+                )
+
+        def px_group(out, lo):
+            for g in range(2):
+                x0 = g * NX + lo
+                nc.tensor.matmul_mx(
+                    out=out,
+                    lhsT=xc[:, x0 : x0 + P].bitcast(FP8X4),
+                    lhsT_scale=xs[:, x0 : x0 + P],
+                    rhs=wc[:, g * CH : g * CH + 256].bitcast(FP8X4),
+                    rhs_scale=wsc[:, g * CH : g * CH + 256],
+                    start=(g == 0),
+                    stop=(g == 1),
+                )
+
+        def pool_pair(src8, dst8, src6, dst6):
+            nc.vector.tensor_reduce(out=dst8, in_=src8, axis=AX.XY, op=ALU.add)
+            nc.vector.tensor_reduce(out=dst6, in_=src6, axis=AX.XY, op=ALU.add)
+
+        def small_vectors():
+            pprm = ps_b.tile([P, P], BF16, tag="B")
+            nc.tensor.transpose(out=pprm[:], in_=prm[:], identity=ident_b[:])
+            prmt = keep.tile([P, 10], F32)
+            nc.vector.tensor_copy(out=prmt[:], in_=pprm[:, 0:10])
+            sc = keep.tile([P, 2], F32)
+            bi = keep.tile([P, 2], F32)
+            nc.vector.tensor_scalar_add(out=sc[:], in0=prmt[:, 8:10], scalar1=EPS)
+            nc.scalar.activation(out=sc[:], in_=sc[:], func=ACT.Sqrt)
+            nc.vector.reciprocal(out=sc[:], in_=sc[:])
+            nc.vector.tensor_mul(out=sc[:], in0=sc[:], in1=prmt[:, 2:4])
+            nc.vector.tensor_sub(out=bi[:], in0=prmt[:, 0:2], in1=prmt[:, 6:8])
+            nc.vector.tensor_mul(out=bi[:], in0=bi[:], in1=sc[:])
+            nc.vector.tensor_add(out=bi[:], in0=bi[:], in1=prmt[:, 4:6])
+            pbv = ps_b.tile([P, 512], F32, tag="B")
+            nc.tensor.matmul(out=pbv[:], lhsT=ones[:], rhs=bvrow[:], start=True, stop=True)
+            bvb = keep.tile([P, 512], F32)
+            nc.scalar.copy(out=bvb[:], in_=pbv[:])
+            return sc, bi, bvb
+
+        sc, bi, bvb = small_vectors()
+
+        for b in range(NB):
+            base = NPX * b
+            pt = ps_t.tile([P, 512], F32, tag="T")
+            pb_v = ps_b.tile([P, 2, P], F32, tag="B")
+            pb_u = ps_b.tile([P, 2, P], F32, tag="B")
+            r_sb = work.tile([P, 2, NPX], F32)
+            vsbs = []
+
+            def chan_v(k):
+                pa = ps_a.tile([P, 512], F32, tag="A")
+                mx_group(pa[:], 2 + k, base, 512)
+                mx_group(pb_v[:, k, :], 2 + k, base + 448, P)
+                pool_pair(
+                    pa[:, 0:504].rearrange("p (g i c j) -> p g c i j", i=3, c=8, j=3),
+                    sums[:, b, k, 46:102].rearrange("p (g c) -> p g c", c=8),
+                    pa[:, 0:480].rearrange("p (g i c j) -> p g c i j", i=4, c=6, j=4),
+                    sums[:, b, k, 10:40].rearrange("p (g c) -> p g c", c=6),
+                )
+
+            def chan_u(k):
+                pa = ps_a.tile([P, 512], F32, tag="A")
+                mx_group(pa[:], 4 + k, base, 512)
+                mx_group(pb_u[:, k, :], 4 + k, base + 448, P)
+                nc.scalar.activation(
+                    out=r_sb[:, k, 0:512], in_=pa[:], func=ACT.Relu,
+                    bias=bi[:, k : k + 1], scale=sc[:, k : k + 1],
+                )
+                nc.scalar.activation(
+                    out=r_sb[:, k, 512:576], in_=pb_u[:, k, 64:128], func=ACT.Relu,
+                    bias=bi[:, k : k + 1], scale=sc[:, k : k + 1],
+                )
+                pool_pair(
+                    r_sb[:, k, :].rearrange("p (g i c j) -> p g c i j", i=3, c=8, j=3),
+                    sums[:, b, 2 + k, 46:110].rearrange("p (g c) -> p g c", c=8),
+                    r_sb[:, k, :].rearrange("p (g i c j) -> p g c i j", i=4, c=6, j=4),
+                    sums[:, b, 2 + k, 10:46].rearrange("p (g c) -> p g c", c=6),
+                )
+
+            def px_mx(m0, m1):
+                px = ps_x.tile([P, 2, 256], F32, tag="X")
+                for m in range(m0, m1):
+                    px_group(px[:, m - m0, :], base + PX_STARTS[m])
+                vsb = vpool.tile([P, 2, 256], F32, tag="vsb")
+                nc.scalar.copy(out=vsb[:, 0 : m1 - m0, :], in_=px[:, 0 : m1 - m0, :])
+                vsbs.append(vsb)
+
+            def px_pool(m0, m1):
+                vsb = vsbs[m0 // 2]
+                for m in range(m0, m1):
+                    nc.tensor.matmul(
+                        out=pt[:, 0:256], lhsT=pmat[:, m, :], rhs=vsb[:, m - m0, :],
+                        start=(m == 0), stop=(m == 4),
+                    )
+
+            def next_x(g, part):
+                if b == 0:
+                    regroup(1, g, 144 * part, 144 * part + 144, False)
+
+            chan_v(0)
+            if b == 0:
+                weight_block(0, False)
+                weight_block(1, False)
+                weight_quant(0, 256)
+            chan_v(1)
+            px_mx(0, 2)
+            if b == 0:
+                weight_block(4, False)
+                weight_block(5, False)
+                weight_quant(512, 768)
+            pool_pair(
+                pb_v[:, :, 56:128].rearrange("p k (i c j) -> p k c i j", i=3, c=8, j=3),
+                sums[:, b, 0:2, 102:110],
+                pb_v[:, :, 32:128].rearrange("p k (i c j) -> p k c i j", i=4, c=6, j=4),
+                sums[:, b, 0:2, 40:46],
+            )
+            next_x(0, 0)
+            px_mx(2, 4)
+            next_x(0, 1)
+            px_pool(0, 2)
+            chan_u(0)
+            next_x(0, 2)
+            px_mx(4, 5)
+            next_x(0, 3)
+            px_pool(2, 4)
+            chan_u(1)
+            next_x(1, 0)
+            next_x(1, 1)
+            px_pool(4, 5)
+            next_x(1, 2)
+            next_x(1, 3)
+            if b == 0:
+                for g in range(2):
+                    quant_x(g, 576, 640)
+                    quant_x(g, 640, 1152)
+            half = work.tile([P, 4, 18], F32)
+            nc.vector.tensor_reduce(
+                out=half[:],
+                in_=sums[:, b, :, 10:46].rearrange("p k (m j) -> p k m j", j=2),
+                axis=AX.X, op=ALU.add,
+            )
+            nc.vector.tensor_reduce(
+                out=sums[:, b, :, 1:10].rearrange("p k (g c) -> p k g c", c=3),
+                in_=half[:].rearrange("p k (g i c) -> p k g c i", i=2, c=3),
+                axis=AX.X, op=ALU.add,
+            )
+            nc.vector.tensor_reduce(
+                out=sums[:, b, :, 0:1], in_=sums[:, b, :, 1:10], axis=AX.X, op=ALU.add
+            )
+            for k in range(2):
+                nc.tensor.transpose(
+                    out=pt[:, 256 + P * k : 384 + P * k], in_=sums[:, b, k, :], identity=ident_f[:]
+                )
+            vo = work.tile([P, 512], F32)
+            nc.vector.scalar_tensor_tensor(
+                out=vo[:], in0=pt[:], scalar=rs[:, 0:1],
+                in1=bvb[:], op0=ALU.mult, op1=ALU.add,
+            )
+            nc.sync.dma_start(out=out_0[b], in_=vo[0:NLOC, :])
+            ko = work.tile([P, 2, NLOC], F32)
+            nc.vector.tensor_tensor(
+                out=ko[:], in0=sums[:, b, 2:4, 0:NLOC],
+                in1=wloc[:].unsqueeze(1).to_broadcast([P, 2, NLOC]), op=ALU.mult,
+            )
+            nc.sync.dma_start(out=out_1[b].rearrange("(k p) l -> p k l", p=P), in_=ko[:])

@@ -29,21 +29,11 @@ def tile_afnb_pa_kernel(tc, low_feats, wk, bk, gk, bek, mk, vk, wv, bv, out_0, o
         keep = ctx.enter_context(tc.tile_pool(name="keep", bufs=1))
         work = ctx.enter_context(tc.tile_pool(name="work", bufs=2))
         vpool = ctx.enter_context(tc.tile_pool(name="vpool", bufs=3))
-        ps_a = ctx.enter_context(tc.psum_pool(name="ps_a", bufs=2))
-        ps_x = ctx.enter_context(tc.psum_pool(name="ps_x", bufs=2))
-        ps_b = ctx.enter_context(tc.psum_pool(name="ps_b", bufs=2))
-        ps_t = ctx.enter_context(tc.psum_pool(name="ps_t", bufs=2))
+        psum = ctx.enter_context(tc.psum_pool(name="psum", bufs=1))
+        ctx.enter_context(tc.manual_schedule())
 
         prm = keep.tile([P, P], BF16)
-        nc.vector.memset(prm[:], 0.0)
         bvrow = keep.tile([P, 512], BF16)
-        nc.vector.memset(bvrow[:], 0.0)
-        for i, vec in enumerate((bk, gk, bek, mk, vk)):
-            nc.scalar.dma_start(
-                out=prm[2 * i : 2 * i + 2, :], in_=vec.rearrange("(r p) -> r p", p=P)
-            )
-        nc.scalar.dma_start(out=bvrow[0:1, :], in_=bv.rearrange("(o c) -> o c", o=1))
-
         w_sb = keep.tile([P, 6 * 1024], BF16)
         xr = []
         for b in range(NB):
@@ -52,6 +42,33 @@ def tile_afnb_pa_kernel(tc, low_feats, wk, bk, gk, bek, mk, vk, wv, bv, out_0, o
                 xr_bg = keep.tile([P, 4, NPX], BF16, name="xr%d%d" % (b, g))
                 row.append(xr_bg)
             xr.append(row)
+        ident_b = keep.tile([P, P], BF16)
+        ident_f = keep.tile([P, P], F32)
+        warm = keep.tile([P, 1], F32)
+        q8 = keep.tile([P, 8, 24], BF16)
+        q6 = keep.tile([P, 6, 24], BF16)
+        q3 = keep.tile([P, 3, 24], BF16)
+        member = keep.tile([P, 24, 24], BF16)
+        mflat = member[:].rearrange("p h w -> p (h w)")
+        mtail = keep.tile([P, P], BF16)
+        pmat = keep.tile([P, 5, P], F32)
+        ones = keep.tile([P, P], BF16)
+        wloc = keep.tile([P, NLOC], F32)
+        rtmp = keep.tile([P, NLOC], F32)
+        rs = keep.tile([P, 1], F32)
+        sums = keep.tile([P, NB, 4, P], F32)
+        prmt = keep.tile([P, 10], F32)
+        sc = keep.tile([P, 2], F32)
+        bi = keep.tile([P, 2], F32)
+        bvb = keep.tile([P, 512], F32)
+        wf = w_sb[:].bitcast(F32)
+        wg = keep.tile([P, 2 * CH * 4], BF16, align_bytes=64)
+        wgf = wg[:].bitcast(F32).rearrange("p (g c u) -> p g c u", g=2, u=2)
+        wc = keep.tile([P, 2 * CH], U32, align_bytes=64)
+        wsc = keep.tile([P, 2 * CH], U8, align_bytes=64)
+        xg = keep.tile([P, 2 * NX * 4], BF16, align_bytes=64)
+        xc = keep.tile([P, 2 * NX], U32, align_bytes=64)
+        xs = keep.tile([P, 2 * NX], U8, align_bytes=64)
 
         def load_x(b, g):
             nc.sync.dma_start(
@@ -67,87 +84,17 @@ def tile_afnb_pa_kernel(tc, low_feats, wk, bk, gk, bek, mk, vk, wv, bv, out_0, o
                 in_=rows.rearrange("(r p) k -> p r k", p=P),
             )
 
-        load_w(2, wv[256:512, :])
-        load_x(0, 0)
-        load_x(0, 1)
-        load_w(0, wv[0:256, :])
-        load_w(4, wk)
-        load_x(1, 0)
-        load_x(1, 1)
-
-        ident_b = keep.tile([P, P], BF16)
-        make_identity(nc, ident_b[:])
-        ident_f = keep.tile([P, P], F32)
-        make_identity(nc, ident_f[:])
-
-        warm = keep.tile([P, 1], F32)
-        nc.vector.memset(warm[:], 1.0)
-        nc.scalar.activation(out=warm[:], in_=warm[:], func=ACT.Sqrt)
-
-        q8 = keep.tile([P, 8, 24], BF16)
-        q6 = keep.tile([P, 6, 24], BF16)
-        q3 = keep.tile([P, 3, 24], BF16)
-        for qt, off, grid, bs in ((q8, 46, 8, 3), (q6, 10, 6, 4), (q3, 1, 3, 8)):
-            nc.vector.tensor_copy(
-                out=qt[:].rearrange("p g (c j) -> p g c j", j=bs),
-                in_=ident_b[:, off : off + grid * grid]
-                .rearrange("p (g c) -> p g c", c=grid)
-                .unsqueeze(3)
-                .to_broadcast([P, grid, grid, bs]),
-            )
-        member = keep.tile([P, 24, 24], BF16)
-        nc.vector.tensor_copy(
-            out=member[:].rearrange("p (g i) w -> p g i w", i=3),
-            in_=q8[:].unsqueeze(2).to_broadcast([P, 8, 3, 24]),
-        )
-        for qt, grid, bs in ((q6, 6, 4), (q3, 3, 8)):
-            mv = member[:].rearrange("p (g i) w -> p g i w", i=bs)
-            nc.vector.tensor_tensor(
-                out=mv, in0=mv, in1=qt[:].unsqueeze(2).to_broadcast([P, grid, bs, 24]), op=ALU.add
-            )
-        mflat = member[:].rearrange("p h w -> p (h w)")
-        nc.vector.tensor_scalar_add(out=mflat, in0=mflat, scalar1=ident_f[:, 0:1])
-        mtail = keep.tile([P, P], BF16)
-        nc.vector.memset(mtail[:], 0.0)
-        nc.vector.tensor_copy(out=mtail[:, 64:128], in_=mflat[:, 512:576])
-        pmem = ps_t.tile([P, 5, P], BF16, tag="T")
-        for m in range(4):
-            nc.tensor.transpose(
-                out=pmem[:, m, :], in_=mflat[:, P * m : P * m + P], identity=ident_b[:]
-            )
-        nc.tensor.transpose(out=pmem[:, 4, :], in_=mtail[:], identity=ident_b[:])
-        pmat = keep.tile([P, 5, P], F32)
-        nc.scalar.copy(out=pmat[:], in_=pmem[:])
-
-        ones = keep.tile([P, P], BF16)
-        nc.vector.memset(ones[:], 1.0)
-        wloc = keep.tile([P, NLOC], F32)
-        nc.vector.memset(wloc[:, 0:1], 576.0)
-        nc.vector.memset(wloc[:, 1:10], 64.0)
-        nc.vector.memset(wloc[:, 10:46], 16.0)
-        nc.vector.memset(wloc[:, 46:110], 9.0)
-        nc.vector.reciprocal(out=wloc[:], in_=wloc[:])
-        rtmp = keep.tile([P, NLOC], F32)
-        nc.vector.tensor_mul(out=rtmp[:], in0=ident_f[:, 0:NLOC], in1=wloc[:])
-        rs = keep.tile([P, 1], F32)
-        nc.vector.tensor_reduce(out=rs[:], in_=rtmp[:], axis=AX.X, op=ALU.add)
-        sums = keep.tile([P, NB, 4, P], F32)
-        nc.vector.memset(sums[:, :, :, NLOC:P], 0.0)
-
-        wf = w_sb[:].bitcast(F32)
-        wg = keep.tile([P, 2 * CH * 4], BF16, align_bytes=64)
-        wgf = wg[:].bitcast(F32).rearrange("p (g c u) -> p g c u", g=2, u=2)
-        wc = keep.tile([P, 2 * CH], U32, align_bytes=64)
-        wsc = keep.tile([P, 2 * CH], U8, align_bytes=64)
-
-        def weight_block(r, on_vector):
-            pw = ps_t.tile([P, 2, 2, P], F32, tag="T")
+        def weight_transposes(r, bank):
+            pw = psum.tile([P, 2, 2, P], F32, tag=bank, name="pw%d" % r)
             for g in range(2):
                 for u in range(2):
                     c0 = 512 * r + 256 * g + 128 * u
                     nc.tensor.transpose(
                         out=pw[:, g, u, :], in_=wf[:, c0 : c0 + P], identity=ident_f[:]
                     )
+            return pw
+
+        def weight_copy(r, pw, on_vector):
             dst = wgf[:, :, P * r : P * r + P, :]
             src = pw[:].rearrange("p g u c -> p g c u")
             if on_vector:
@@ -164,10 +111,6 @@ def tile_afnb_pa_kernel(tc, low_feats, wk, bk, gk, bek, mk, vk, wv, bv, out_0, o
                     scales=wsc[:, lo:hi],
                     in_=wg[:, 4 * lo : 4 * hi],
                 )
-
-        xg = keep.tile([P, 2 * NX * 4], BF16, align_bytes=64)
-        xc = keep.tile([P, 2 * NX], U32, align_bytes=64)
-        xs = keep.tile([P, 2 * NX], U8, align_bytes=64)
 
         def regroup(b, g, a0, a1, on_vector):
             base = g * NX + NPX * b
@@ -188,18 +131,6 @@ def tile_afnb_pa_kernel(tc, low_feats, wk, bk, gk, bek, mk, vk, wv, bv, out_0, o
                 scales=xs[:, lo:hi],
                 in_=xg[:, 4 * lo : 4 * hi],
             )
-
-        weight_block(2, False)
-        weight_block(3, True)
-        regroup(0, 0, 0, 384, True)
-        regroup(0, 0, 384, 576, False)
-        weight_quant(256, 512)
-        quant_x(0, 0, 512)
-        quant_x(0, 512, 576)
-        regroup(0, 1, 0, 384, True)
-        regroup(0, 1, 384, 576, False)
-        quant_x(1, 0, 512)
-        quant_x(1, 512, 576)
 
         def mx_group(out, blk, lo, n):
             for g in range(2):
@@ -232,123 +163,172 @@ def tile_afnb_pa_kernel(tc, low_feats, wk, bk, gk, bek, mk, vk, wv, bv, out_0, o
             nc.vector.tensor_reduce(out=dst8, in_=src8, axis=AX.XY, op=ALU.add)
             nc.vector.tensor_reduce(out=dst6, in_=src6, axis=AX.XY, op=ALU.add)
 
-        def small_vectors():
-            pprm = ps_b.tile([P, P], BF16, tag="B")
-            nc.tensor.transpose(out=pprm[:], in_=prm[:], identity=ident_b[:])
-            prmt = keep.tile([P, 10], F32)
-            nc.vector.tensor_copy(out=prmt[:], in_=pprm[:, 0:10])
-            sc = keep.tile([P, 2], F32)
-            bi = keep.tile([P, 2], F32)
-            nc.vector.tensor_scalar_add(out=sc[:], in0=prmt[:, 8:10], scalar1=EPS)
-            nc.scalar.activation(out=sc[:], in_=sc[:], func=ACT.Sqrt)
-            nc.vector.reciprocal(out=sc[:], in_=sc[:])
-            nc.vector.tensor_mul(out=sc[:], in0=sc[:], in1=prmt[:, 2:4])
-            nc.vector.tensor_sub(out=bi[:], in0=prmt[:, 0:2], in1=prmt[:, 6:8])
-            nc.vector.tensor_mul(out=bi[:], in0=bi[:], in1=sc[:])
-            nc.vector.tensor_add(out=bi[:], in0=bi[:], in1=prmt[:, 4:6])
-            pbv = ps_b.tile([P, 512], F32, tag="B")
-            nc.tensor.matmul(out=pbv[:], lhsT=ones[:], rhs=bvrow[:], start=True, stop=True)
-            bvb = keep.tile([P, 512], F32)
-            nc.scalar.copy(out=bvb[:], in_=pbv[:])
-            return sc, bi, bvb
+        nc.vector.memset(prm[:], 0.0)
+        nc.vector.memset(bvrow[:], 0.0)
+        for i, vec in enumerate((bk, gk, bek, mk, vk)):
+            nc.scalar.dma_start(
+                out=prm[2 * i : 2 * i + 2, :], in_=vec.rearrange("(r p) -> r p", p=P)
+            )
+        nc.scalar.dma_start(out=bvrow[0:1, :], in_=bv.rearrange("(o c) -> o c", o=1))
+        load_w(2, wv[256:512, :])
+        load_x(0, 0)
+        load_x(0, 1)
+        load_w(0, wv[0:256, :])
+        load_w(4, wk)
+        load_x(1, 0)
+        load_x(1, 1)
+        make_identity(nc, ident_b[:])
+        make_identity(nc, ident_f[:])
+        nc.vector.memset(warm[:], 1.0)
+        nc.scalar.activation(out=warm[:], in_=warm[:], func=ACT.Sqrt)
 
-        sc, bi, bvb = small_vectors()
+        for qt, off, grid, bs in ((q8, 46, 8, 3), (q6, 10, 6, 4), (q3, 1, 3, 8)):
+            nc.vector.tensor_copy(
+                out=qt[:].rearrange("p g (c j) -> p g c j", j=bs),
+                in_=ident_b[:, off : off + grid * grid]
+                .rearrange("p (g c) -> p g c", c=grid)
+                .unsqueeze(3)
+                .to_broadcast([P, grid, grid, bs]),
+            )
+        nc.vector.tensor_copy(
+            out=member[:].rearrange("p (g i) w -> p g i w", i=3),
+            in_=q8[:].unsqueeze(2).to_broadcast([P, 8, 3, 24]),
+        )
+        for qt, grid, bs in ((q6, 6, 4), (q3, 3, 8)):
+            mv = member[:].rearrange("p (g i) w -> p g i w", i=bs)
+            nc.vector.tensor_tensor(
+                out=mv, in0=mv, in1=qt[:].unsqueeze(2).to_broadcast([P, grid, bs, 24]), op=ALU.add
+            )
+        nc.vector.tensor_scalar_add(out=mflat, in0=mflat, scalar1=ident_f[:, 0:1])
+        nc.vector.memset(mtail[:], 0.0)
+        nc.vector.tensor_copy(out=mtail[:, 64:128], in_=mflat[:, 512:576])
+        nc.vector.memset(ones[:], 1.0)
+        nc.vector.memset(wloc[:, 0:1], 576.0)
+        nc.vector.memset(wloc[:, 1:10], 64.0)
+        nc.vector.memset(wloc[:, 10:46], 16.0)
+        nc.vector.memset(wloc[:, 46:110], 9.0)
+        nc.vector.reciprocal(out=wloc[:], in_=wloc[:])
+        nc.vector.tensor_mul(out=rtmp[:], in0=ident_f[:, 0:NLOC], in1=wloc[:])
+        nc.vector.tensor_reduce(out=rs[:], in_=rtmp[:], axis=AX.X, op=ALU.add)
+        nc.vector.memset(sums[:, :, :, NLOC:P], 0.0)
 
-        for b in range(NB):
-            base = NPX * b
-            pt = ps_t.tile([P, 512], F32, tag="T")
-            pb_v = ps_b.tile([P, 2, P], F32, tag="B")
-            pb_u = ps_b.tile([P, 2, P], F32, tag="B")
-            r_sb = work.tile([P, 2, NPX], F32)
-            vsbs = []
+        pw2 = weight_transposes(2, "A0")
+        pw3 = weight_transposes(3, "A1")
+        weight_copy(2, pw2, False)
+        weight_copy(3, pw3, True)
+        pmem = psum.tile([P, 5, P], BF16, tag="B0")
+        for m in range(4):
+            nc.tensor.transpose(
+                out=pmem[:, m, :], in_=mflat[:, P * m : P * m + P], identity=ident_b[:]
+            )
+        nc.tensor.transpose(out=pmem[:, 4, :], in_=mtail[:], identity=ident_b[:])
+        pprm = psum.tile([P, P], BF16, tag="B1")
+        nc.tensor.transpose(out=pprm[:], in_=prm[:], identity=ident_b[:])
 
-            def chan_v(k):
-                pa = ps_a.tile([P, 512], F32, tag="A")
-                mx_group(pa[:], 2 + k, base, 512)
-                mx_group(pb_v[:, k, :], 2 + k, base + 448, P)
-                pool_pair(
-                    pa[:, 0:504].rearrange("p (g i c j) -> p g c i j", i=3, c=8, j=3),
-                    sums[:, b, k, 46:102].rearrange("p (g c) -> p g c", c=8),
-                    pa[:, 0:480].rearrange("p (g i c j) -> p g c i j", i=4, c=6, j=4),
-                    sums[:, b, k, 10:40].rearrange("p (g c) -> p g c", c=6),
-                )
+        regroup(0, 0, 0, 384, True)
+        regroup(0, 0, 384, 576, False)
+        weight_quant(256, 512)
+        nc.scalar.copy(out=pmat[:], in_=pmem[:])
+        nc.vector.tensor_copy(out=prmt[:], in_=pprm[:, 0:10])
+        nc.vector.tensor_scalar_add(out=sc[:], in0=prmt[:, 8:10], scalar1=EPS)
+        pbv = psum.tile([P, 512], F32, tag="B1")
+        nc.tensor.matmul(out=pbv[:], lhsT=ones[:], rhs=bvrow[:], start=True, stop=True)
+        quant_x(0, 0, 512)
+        quant_x(0, 512, 576)
+        regroup(0, 1, 0, 384, True)
+        regroup(0, 1, 384, 576, False)
+        nc.scalar.activation(out=sc[:], in_=sc[:], func=ACT.Sqrt)
+        nc.scalar.copy(out=bvb[:], in_=pbv[:])
+        quant_x(1, 0, 512)
+        quant_x(1, 512, 576)
+        pw0 = weight_transposes(0, "X0")
+        pw1 = weight_transposes(1, "X1")
+        weight_copy(0, pw0, False)
+        weight_copy(1, pw1, False)
+        weight_quant(0, 256)
+        nc.vector.reciprocal(out=sc[:], in_=sc[:])
+        nc.vector.tensor_mul(out=sc[:], in0=sc[:], in1=prmt[:, 2:4])
+        nc.vector.tensor_sub(out=bi[:], in0=prmt[:, 0:2], in1=prmt[:, 6:8])
+        nc.vector.tensor_mul(out=bi[:], in0=bi[:], in1=sc[:])
+        nc.vector.tensor_add(out=bi[:], in0=bi[:], in1=prmt[:, 4:6])
+        pw4 = weight_transposes(4, "T0")
+        pw5 = weight_transposes(5, "T1")
+        weight_copy(4, pw4, False)
+        weight_copy(5, pw5, False)
 
-            def chan_u(k):
-                pa = ps_a.tile([P, 512], F32, tag="A")
-                mx_group(pa[:], 4 + k, base, 512)
-                mx_group(pb_u[:, k, :], 4 + k, base + 448, P)
-                nc.scalar.activation(
-                    out=r_sb[:, k, 0:512], in_=pa[:], func=ACT.Relu,
-                    bias=bi[:, k : k + 1], scale=sc[:, k : k + 1],
-                )
-                nc.scalar.activation(
-                    out=r_sb[:, k, 512:576], in_=pb_u[:, k, 64:128], func=ACT.Relu,
-                    bias=bi[:, k : k + 1], scale=sc[:, k : k + 1],
-                )
-                pool_pair(
-                    r_sb[:, k, :].rearrange("p (g i c j) -> p g c i j", i=3, c=8, j=3),
-                    sums[:, b, 2 + k, 46:110].rearrange("p (g c) -> p g c", c=8),
-                    r_sb[:, k, :].rearrange("p (g i c j) -> p g c i j", i=4, c=6, j=4),
-                    sums[:, b, 2 + k, 10:46].rearrange("p (g c) -> p g c", c=6),
-                )
+        state = {}
 
-            def px_mx(m0, m1):
-                px = ps_x.tile([P, 2, 256], F32, tag="X")
-                for m in range(m0, m1):
-                    px_group(px[:, m - m0, :], base + PX_STARTS[m])
-                vsb = vpool.tile([P, 2, 256], F32, tag="vsb")
-                nc.scalar.copy(out=vsb[:, 0 : m1 - m0, :], in_=px[:, 0 : m1 - m0, :])
-                vsbs.append(vsb)
+        def begin(b):
+            state["pt", b] = psum.tile([P, 512], F32, tag="T%d" % b, name="pt%d" % b)
+            state["pbv", b] = psum.tile([P, 2, P], F32, tag="B0", name="pb_v%d" % b)
+            state["pbu", b] = psum.tile([P, 2, P], F32, tag="B1", name="pb_u%d" % b)
+            state["r", b] = work.tile([P, 2, NPX], F32, tag="r_sb", name="r_sb%d" % b)
 
-            def px_pool(m0, m1):
-                vsb = vsbs[m0 // 2]
-                for m in range(m0, m1):
-                    nc.tensor.matmul(
-                        out=pt[:, 0:256], lhsT=pmat[:, m, :], rhs=vsb[:, m - m0, :],
-                        start=(m == 0), stop=(m == 4),
-                    )
+        def v_mx(b, k, bank):
+            pa = psum.tile([P, 512], F32, tag=bank, name="pav%d%d" % (b, k))
+            mx_group(pa[:], 2 + k, NPX * b, 512)
+            mx_group(state["pbv", b][:, k, :], 2 + k, NPX * b + 448, P)
+            state["pav", b, k] = pa
 
-            def next_x(g, part):
-                if b == 0:
-                    regroup(1, g, 144 * part, 144 * part + 144, False)
+        def v_pool(b, k):
+            pa = state["pav", b, k]
+            pool_pair(
+                pa[:, 0:504].rearrange("p (g i c j) -> p g c i j", i=3, c=8, j=3),
+                sums[:, b, k, 46:102].rearrange("p (g c) -> p g c", c=8),
+                pa[:, 0:480].rearrange("p (g i c j) -> p g c i j", i=4, c=6, j=4),
+                sums[:, b, k, 10:40].rearrange("p (g c) -> p g c", c=6),
+            )
 
-            chan_v(0)
-            if b == 0:
-                weight_block(0, False)
-                weight_block(1, False)
-                weight_quant(0, 256)
-            chan_v(1)
-            px_mx(0, 2)
-            if b == 0:
-                weight_block(4, False)
-                weight_block(5, False)
-                weight_quant(512, 768)
+        def v_pool_tail(b):
+            pb_v = state["pbv", b]
             pool_pair(
                 pb_v[:, :, 56:128].rearrange("p k (i c j) -> p k c i j", i=3, c=8, j=3),
                 sums[:, b, 0:2, 102:110],
                 pb_v[:, :, 32:128].rearrange("p k (i c j) -> p k c i j", i=4, c=6, j=4),
                 sums[:, b, 0:2, 40:46],
             )
-            next_x(0, 0)
-            px_mx(2, 4)
-            next_x(0, 1)
-            px_pool(0, 2)
-            chan_u(0)
-            next_x(0, 2)
-            px_mx(4, 5)
-            next_x(0, 3)
-            px_pool(2, 4)
-            chan_u(1)
-            next_x(1, 0)
-            next_x(1, 1)
-            px_pool(4, 5)
-            next_x(1, 2)
-            next_x(1, 3)
-            if b == 0:
-                for g in range(2):
-                    quant_x(g, 576, 640)
-                    quant_x(g, 640, 1152)
-            half = work.tile([P, 4, 18], F32)
+
+        def u_mx(b, k, bank):
+            pa = psum.tile([P, 512], F32, tag=bank, name="pau%d%d" % (b, k))
+            mx_group(pa[:], 4 + k, NPX * b, 512)
+            mx_group(state["pbu", b][:, k, :], 4 + k, NPX * b + 448, P)
+            r_sb = state["r", b]
+            nc.scalar.activation(
+                out=r_sb[:, k, 0:512], in_=pa[:], func=ACT.Relu,
+                bias=bi[:, k : k + 1], scale=sc[:, k : k + 1],
+            )
+            nc.scalar.activation(
+                out=r_sb[:, k, 512:576], in_=state["pbu", b][:, k, 64:128], func=ACT.Relu,
+                bias=bi[:, k : k + 1], scale=sc[:, k : k + 1],
+            )
+
+        def u_pool(b, k):
+            r_sb = state["r", b]
+            pool_pair(
+                r_sb[:, k, :].rearrange("p (g i c j) -> p g c i j", i=3, c=8, j=3),
+                sums[:, b, 2 + k, 46:110].rearrange("p (g c) -> p g c", c=8),
+                r_sb[:, k, :].rearrange("p (g i c j) -> p g c i j", i=4, c=6, j=4),
+                sums[:, b, 2 + k, 10:46].rearrange("p (g c) -> p g c", c=6),
+            )
+
+        def px_mx(b, m0, m1, bank):
+            px = psum.tile([P, 2, 256], F32, tag=bank, name="px%d%d" % (b, m0))
+            for m in range(m0, m1):
+                px_group(px[:, m - m0, :], NPX * b + PX_STARTS[m])
+            vsb = vpool.tile([P, 2, 256], F32, tag="vsb", name="vsb%d%d" % (b, m0))
+            nc.scalar.copy(out=vsb[:, 0 : m1 - m0, :], in_=px[:, 0 : m1 - m0, :])
+            state["vsb", b, m0] = vsb
+
+        def px_pool(b, m0, m1):
+            vsb = state["vsb", b, m0]
+            for m in range(m0, m1):
+                nc.tensor.matmul(
+                    out=state["pt", b][:, 0:256], lhsT=pmat[:, m, :], rhs=vsb[:, m - m0, :],
+                    start=(m == 0), stop=(m == 4),
+                )
+
+        def coarse_grids(b):
+            half = work.tile([P, 4, 18], F32, tag="half", name="half%d" % b)
             nc.vector.tensor_reduce(
                 out=half[:],
                 in_=sums[:, b, :, 10:46].rearrange("p k (m j) -> p k m j", j=2),
@@ -362,19 +342,72 @@ def tile_afnb_pa_kernel(tc, low_feats, wk, bk, gk, bek, mk, vk, wv, bv, out_0, o
             nc.vector.tensor_reduce(
                 out=sums[:, b, :, 0:1], in_=sums[:, b, :, 1:10], axis=AX.X, op=ALU.add
             )
+
+        def value_transposes(b):
             for k in range(2):
                 nc.tensor.transpose(
-                    out=pt[:, 256 + P * k : 384 + P * k], in_=sums[:, b, k, :], identity=ident_f[:]
+                    out=state["pt", b][:, 256 + P * k : 384 + P * k], in_=sums[:, b, k, :],
+                    identity=ident_f[:],
                 )
-            vo = work.tile([P, 512], F32)
+
+        def finish(b):
+            vo = work.tile([P, 512], F32, tag="vo", name="vo%d" % b)
             nc.vector.scalar_tensor_tensor(
-                out=vo[:], in0=pt[:], scalar=rs[:, 0:1],
+                out=vo[:], in0=state["pt", b][:], scalar=rs[:, 0:1],
                 in1=bvb[:], op0=ALU.mult, op1=ALU.add,
             )
             nc.sync.dma_start(out=out_0[b], in_=vo[0:NLOC, :])
-            ko = work.tile([P, 2, NLOC], F32)
+            ko = work.tile([P, 2, NLOC], F32, tag="ko", name="ko%d" % b)
             nc.vector.tensor_tensor(
                 out=ko[:], in0=sums[:, b, 2:4, 0:NLOC],
                 in1=wloc[:].unsqueeze(1).to_broadcast([P, 2, NLOC]), op=ALU.mult,
             )
             nc.sync.dma_start(out=out_1[b].rearrange("(k p) l -> p k l", p=P), in_=ko[:])
+
+        begin(0)
+        v_mx(0, 0, "A0")
+        v_mx(0, 1, "A1")
+        v_pool(0, 0)
+        weight_quant(512, 768)
+        regroup(1, 0, 384, 576, False)
+        px_mx(0, 0, 2, "X0")
+        px_mx(0, 2, 4, "X1")
+        v_pool(0, 1)
+        v_pool_tail(0)
+        u_mx(0, 0, "A0")
+        px_pool(0, 0, 2)
+        regroup(1, 0, 0, 384, True)
+        regroup(1, 1, 384, 576, False)
+        u_mx(0, 1, "A1")
+        u_pool(0, 0)
+        px_mx(0, 4, 5, "X0")
+        px_pool(0, 2, 4)
+        regroup(1, 1, 0, 384, True)
+        u_pool(0, 1)
+        px_pool(0, 4, 5)
+        for g in range(2):
+            quant_x(g, 576, 640)
+            quant_x(g, 640, 1152)
+        coarse_grids(0)
+
+        begin(1)
+        v_mx(1, 0, "A0")
+        u_mx(1, 0, "A1")
+        value_transposes(0)
+        v_pool(1, 0)
+        finish(0)
+        px_mx(1, 0, 2, "X0")
+        px_mx(1, 2, 4, "X1")
+        v_mx(1, 1, "A1")
+        u_mx(1, 1, "A0")
+        u_pool(1, 0)
+        px_pool(1, 0, 2)
+        px_mx(1, 4, 5, "X0")
+        v_pool(1, 1)
+        px_pool(1, 2, 4)
+        px_pool(1, 4, 5)
+        u_pool(1, 1)
+        v_pool_tail(1)
+        coarse_grids(1)
+        value_transposes(1)
+        finish(1)

@@ -118,7 +118,11 @@ def tile_afnb_pa_kernel(tc, low_feats, wk, bk, gk, bek, mk, vk, wv, bv, out_0, o
                 "p (c i t) -> p c t i", i=4, t=4
             )
             src = xr[b][g][:, :, a0:a1].rearrange("p t (c i) -> p c t i", i=4)
-            if on_vector:
+            if on_vector == "gpsimd":
+                nc.gpsimd.tensor_scalar(
+                    out=dst, in0=src, scalar1=1.0, scalar2=0.0, op0=ALU.mult, op1=ALU.add
+                )
+            elif on_vector:
                 nc.vector.tensor_copy(out=dst, in_=src)
             else:
                 nc.scalar.copy(out=dst, in_=src)
@@ -228,7 +232,6 @@ def tile_afnb_pa_kernel(tc, low_feats, wk, bk, gk, bek, mk, vk, wv, bv, out_0, o
         regroup(0, 0, 0, 384, True)
         regroup(0, 0, 384, 576, False)
         weight_quant(256, 512)
-        nc.scalar.copy(out=pmat[:], in_=pmem[:])
         nc.vector.tensor_copy(out=prmt[:], in_=pprm[:, 0:10])
         nc.vector.tensor_scalar_add(out=sc[:], in0=prmt[:, 8:10], scalar1=EPS)
         pbv = psum.tile([P, 512], F32, tag="B1")
@@ -237,6 +240,7 @@ def tile_afnb_pa_kernel(tc, low_feats, wk, bk, gk, bek, mk, vk, wv, bv, out_0, o
         quant_x(0, 512, 576)
         regroup(0, 1, 0, 384, True)
         regroup(0, 1, 384, 576, False)
+        nc.scalar.copy(out=pmat[:], in_=pmem[:])
         nc.scalar.activation(out=sc[:], in_=sc[:], func=ACT.Sqrt)
         nc.scalar.copy(out=bvb[:], in_=pbv[:])
         quant_x(1, 0, 512)
@@ -311,6 +315,36 @@ def tile_afnb_pa_kernel(tc, low_feats, wk, bk, gk, bek, mk, vk, wv, bv, out_0, o
                 sums[:, b, 2 + k, 10:46].rearrange("p (g c) -> p g c", c=6),
             )
 
+        def u_pool_gpsimd(b, k):
+            r_k = state["r", b][:, k, :]
+            add = ALU.add
+            tg = "%d%d" % (b, k)
+            rv3 = r_k.rearrange("p (m j) -> p m j", j=3)
+            t8 = work.tile([P, 192], F32, tag="t8", name="t8_" + tg)
+            nc.gpsimd.tensor_tensor(out=t8[:], in0=rv3[:, :, 0], in1=rv3[:, :, 1], op=add)
+            nc.gpsimd.tensor_tensor(out=t8[:], in0=t8[:], in1=rv3[:, :, 2], op=add)
+            t8v = t8[:].rearrange("p (g i c) -> p g i c", i=3, c=8)
+            u8 = work.tile([P, 8, 8], F32, tag="u8", name="u8_" + tg)
+            nc.gpsimd.tensor_tensor(out=u8[:], in0=t8v[:, :, 0, :], in1=t8v[:, :, 1, :], op=add)
+            nc.gpsimd.tensor_tensor(
+                out=sums[:, b, 2 + k, 46:110].rearrange("p (g c) -> p g c", c=8),
+                in0=u8[:], in1=t8v[:, :, 2, :], op=add,
+            )
+            rv2 = r_k.rearrange("p (m j) -> p m j", j=2)
+            p6 = work.tile([P, 288], F32, tag="p6", name="p6_" + tg)
+            nc.gpsimd.tensor_tensor(out=p6[:], in0=rv2[:, :, 0], in1=rv2[:, :, 1], op=add)
+            p6v = p6[:].rearrange("p (m j) -> p m j", j=2)
+            p6b = work.tile([P, 144], F32, tag="p6b", name="p6b_" + tg)
+            nc.gpsimd.tensor_tensor(out=p6b[:], in0=p6v[:, :, 0], in1=p6v[:, :, 1], op=add)
+            p6bv = p6b[:].rearrange("p (a e c) -> p a e c", e=2, c=6)
+            h6 = work.tile([P, 12, 6], F32, tag="h6", name="h6_" + tg)
+            nc.gpsimd.tensor_tensor(out=h6[:], in0=p6bv[:, :, 0, :], in1=p6bv[:, :, 1, :], op=add)
+            h6v = h6[:].rearrange("p (g a) c -> p g a c", a=2)
+            nc.gpsimd.tensor_tensor(
+                out=sums[:, b, 2 + k, 10:46].rearrange("p (g c) -> p g c", c=6),
+                in0=h6v[:, :, 0, :], in1=h6v[:, :, 1, :], op=add,
+            )
+
         def px_mx(b, m0, m1, bank):
             px = psum.tile([P, 2, 256], F32, tag=bank, name="px%d%d" % (b, m0))
             for m in range(m0, m1):
@@ -327,20 +361,22 @@ def tile_afnb_pa_kernel(tc, low_feats, wk, bk, gk, bek, mk, vk, wv, bv, out_0, o
                     start=(m == 0), stop=(m == 4),
                 )
 
-        def coarse_grids(b):
-            half = work.tile([P, 4, 18], F32, tag="half", name="half%d" % b)
+        rows = sums[:].rearrange("p b q l -> p (b q) l")
+
+        def coarse_grids(q0, q1):
+            half = work.tile([P, q1 - q0, 18], F32, tag="half%d" % q0, name="half%d" % q0)
             nc.vector.tensor_reduce(
                 out=half[:],
-                in_=sums[:, b, :, 10:46].rearrange("p k (m j) -> p k m j", j=2),
+                in_=rows[:, q0:q1, 10:46].rearrange("p k (m j) -> p k m j", j=2),
                 axis=AX.X, op=ALU.add,
             )
             nc.vector.tensor_reduce(
-                out=sums[:, b, :, 1:10].rearrange("p k (g c) -> p k g c", c=3),
+                out=rows[:, q0:q1, 1:10].rearrange("p k (g c) -> p k g c", c=3),
                 in_=half[:].rearrange("p k (g i c) -> p k g c i", i=2, c=3),
                 axis=AX.X, op=ALU.add,
             )
             nc.vector.tensor_reduce(
-                out=sums[:, b, :, 0:1], in_=sums[:, b, :, 1:10], axis=AX.X, op=ALU.add
+                out=rows[:, q0:q1, 0:1], in_=rows[:, q0:q1, 1:10], axis=AX.X, op=ALU.add
             )
 
         def value_transposes(b):
@@ -350,52 +386,59 @@ def tile_afnb_pa_kernel(tc, low_feats, wk, bk, gk, bek, mk, vk, wv, bv, out_0, o
                     identity=ident_f[:],
                 )
 
-        def finish(b):
+        def finish_value(b):
             vo = work.tile([P, 512], F32, tag="vo", name="vo%d" % b)
             nc.vector.scalar_tensor_tensor(
                 out=vo[:], in0=state["pt", b][:], scalar=rs[:, 0:1],
                 in1=bvb[:], op0=ALU.mult, op1=ALU.add,
             )
             nc.sync.dma_start(out=out_0[b], in_=vo[0:NLOC, :])
-            ko = work.tile([P, 2, NLOC], F32, tag="ko", name="ko%d" % b)
-            nc.vector.tensor_tensor(
-                out=ko[:], in0=sums[:, b, 2:4, 0:NLOC],
-                in1=wloc[:].unsqueeze(1).to_broadcast([P, 2, NLOC]), op=ALU.mult,
+
+        def finish_keys():
+            ko = keep.tile([P, NB, 2, NLOC], F32)
+            nc.gpsimd.tensor_tensor(
+                out=ko[:], in0=sums[:, :, 2:4, 0:NLOC],
+                in1=wloc[:].unsqueeze(1).unsqueeze(1).to_broadcast([P, NB, 2, NLOC]), op=ALU.mult,
             )
-            nc.sync.dma_start(out=out_1[b].rearrange("(k p) l -> p k l", p=P), in_=ko[:])
+            for b in range(NB):
+                nc.sync.dma_start(
+                    out=out_1[b].rearrange("(k p) l -> p k l", p=P), in_=ko[:, b, :, :]
+                )
 
         begin(0)
         v_mx(0, 0, "A0")
         v_mx(0, 1, "A1")
         v_pool(0, 0)
         weight_quant(512, 768)
-        regroup(1, 0, 384, 576, False)
         px_mx(0, 0, 2, "X0")
         px_mx(0, 2, 4, "X1")
+        regroup(1, 0, 192, 384, "gpsimd")
+        regroup(1, 0, 384, 576, False)
         v_pool(0, 1)
-        v_pool_tail(0)
-        u_mx(0, 0, "A0")
         px_pool(0, 0, 2)
-        regroup(1, 0, 0, 384, True)
-        regroup(1, 1, 384, 576, False)
-        u_mx(0, 1, "A1")
-        u_pool(0, 0)
+        u_mx(0, 0, "A0")
         px_mx(0, 4, 5, "X0")
+        regroup(1, 1, 192, 384, "gpsimd")
+        regroup(1, 1, 384, 576, False)
         px_pool(0, 2, 4)
-        regroup(1, 1, 0, 384, True)
-        u_pool(0, 1)
+        u_mx(0, 1, "A1")
+        u_pool_gpsimd(0, 0)
         px_pool(0, 4, 5)
+        regroup(1, 0, 0, 192, True)
+        regroup(1, 1, 0, 192, True)
+        u_pool_gpsimd(0, 1)
         for g in range(2):
             quant_x(g, 576, 640)
             quant_x(g, 640, 1152)
-        coarse_grids(0)
+        v_pool_tail(0)
+        coarse_grids(0, 2)
 
         begin(1)
         v_mx(1, 0, "A0")
         u_mx(1, 0, "A1")
         value_transposes(0)
         v_pool(1, 0)
-        finish(0)
+        finish_value(0)
         px_mx(1, 0, 2, "X0")
         px_mx(1, 2, 4, "X1")
         v_mx(1, 1, "A1")
@@ -408,6 +451,7 @@ def tile_afnb_pa_kernel(tc, low_feats, wk, bk, gk, bek, mk, vk, wv, bv, out_0, o
         px_pool(1, 4, 5)
         u_pool(1, 1)
         v_pool_tail(1)
-        coarse_grids(1)
+        coarse_grids(2, 8)
         value_transposes(1)
-        finish(1)
+        finish_keys()
+        finish_value(1)

@@ -78,9 +78,11 @@ def tile_afnb_pa_kernel(tc, low_feats, wk, bk, gk, bek, mk, vk, wv, bv, out_0, o
                 ),
             )
 
-        def load_w(r0, rows):
+        def load_w(r0, n_blocks, rows):
             nc.sync.dma_start(
-                out=w_sb[:, 1024 * r0 : 1024 * (r0 + 2)].rearrange("p (r k) -> p r k", k=1024),
+                out=w_sb[:, 1024 * r0 : 1024 * (r0 + n_blocks)].rearrange(
+                    "p (r k) -> p r k", k=1024
+                ),
                 in_=rows.rearrange("(r p) k -> p r k", p=P),
             )
 
@@ -169,21 +171,23 @@ def tile_afnb_pa_kernel(tc, low_feats, wk, bk, gk, bek, mk, vk, wv, bv, out_0, o
 
         nc.vector.memset(prm[:], 0.0)
         nc.vector.memset(bvrow[:], 0.0)
+        nc.vector.memset(ones[:], 1.0)
+        nc.vector.memset(warm[:], 1.0)
         for i, vec in enumerate((bk, gk, bek, mk, vk)):
             nc.scalar.dma_start(
                 out=prm[2 * i : 2 * i + 2, :], in_=vec.rearrange("(r p) -> r p", p=P)
             )
         nc.scalar.dma_start(out=bvrow[0:1, :], in_=bv.rearrange("(o c) -> o c", o=1))
-        load_w(2, wv[256:512, :])
         load_x(0, 0)
+        load_w(2, 1, wv[256:384, :])
         load_x(0, 1)
-        load_w(0, wv[0:256, :])
-        load_w(4, wk)
+        load_w(3, 1, wv[384:512, :])
+        load_w(0, 2, wv[0:256, :])
+        load_w(4, 2, wk)
         load_x(1, 0)
         load_x(1, 1)
         make_identity(nc, ident_b[:])
         make_identity(nc, ident_f[:])
-        nc.vector.memset(warm[:], 1.0)
         nc.scalar.activation(out=warm[:], in_=warm[:], func=ACT.Sqrt)
 
         for qt, off, grid, bs in ((q8, 46, 8, 3), (q6, 10, 6, 4), (q3, 1, 3, 8)):
@@ -206,7 +210,6 @@ def tile_afnb_pa_kernel(tc, low_feats, wk, bk, gk, bek, mk, vk, wv, bv, out_0, o
         nc.vector.tensor_scalar_add(out=mflat, in0=mflat, scalar1=ident_f[:, 0:1])
         nc.vector.memset(mtail[:], 0.0)
         nc.vector.tensor_copy(out=mtail[:, 64:128], in_=mflat[:, 512:576])
-        nc.vector.memset(ones[:], 1.0)
         nc.vector.memset(wloc[:, 0:1], 576.0)
         nc.vector.memset(wloc[:, 1:10], 64.0)
         nc.vector.memset(wloc[:, 10:46], 16.0)
@@ -216,49 +219,45 @@ def tile_afnb_pa_kernel(tc, low_feats, wk, bk, gk, bek, mk, vk, wv, bv, out_0, o
         nc.vector.tensor_reduce(out=rs[:], in_=rtmp[:], axis=AX.X, op=ALU.add)
         nc.vector.memset(sums[:, :, :, NLOC:P], 0.0)
 
-        pw2 = weight_transposes(2, "A0")
-        pw3 = weight_transposes(3, "A1")
-        weight_copy(2, pw2, False)
-        weight_copy(3, pw3, True)
+        pbv = psum.tile([P, 512], F32, tag="T1")
+        nc.tensor.matmul(out=pbv[:], lhsT=ones[:], rhs=bvrow[:], start=True, stop=True)
+        pprm = psum.tile([P, P], BF16, tag="B1")
+        nc.tensor.transpose(out=pprm[:], in_=prm[:], identity=ident_b[:])
         pmem = psum.tile([P, 5, P], BF16, tag="B0")
         for m in range(4):
             nc.tensor.transpose(
                 out=pmem[:, m, :], in_=mflat[:, P * m : P * m + P], identity=ident_b[:]
             )
         nc.tensor.transpose(out=pmem[:, 4, :], in_=mtail[:], identity=ident_b[:])
-        pprm = psum.tile([P, P], BF16, tag="B1")
-        nc.tensor.transpose(out=pprm[:], in_=prm[:], identity=ident_b[:])
+        nc.scalar.copy(out=bvb[:], in_=pbv[:])
+        nc.vector.tensor_copy(out=prmt[:], in_=pprm[:, 0:10])
+        nc.vector.tensor_scalar_add(out=sc[:], in0=prmt[:, 8:10], scalar1=EPS)
+        nc.scalar.activation(out=sc[:], in_=sc[:], func=ACT.Sqrt)
 
         regroup(0, 0, 0, 384, True)
         regroup(0, 0, 384, 576, False)
-        weight_quant(256, 512)
-        nc.vector.tensor_copy(out=prmt[:], in_=pprm[:, 0:10])
-        nc.vector.tensor_scalar_add(out=sc[:], in0=prmt[:, 8:10], scalar1=EPS)
-        pbv = psum.tile([P, 512], F32, tag="B1")
-        nc.tensor.matmul(out=pbv[:], lhsT=ones[:], rhs=bvrow[:], start=True, stop=True)
-        quant_x(0, 0, 512)
-        quant_x(0, 512, 576)
-        regroup(0, 1, 0, 384, True)
-        regroup(0, 1, 384, 576, False)
-        nc.scalar.copy(out=pmat[:], in_=pmem[:])
-        nc.scalar.activation(out=sc[:], in_=sc[:], func=ACT.Sqrt)
-        nc.scalar.copy(out=bvb[:], in_=pbv[:])
-        quant_x(1, 0, 512)
-        quant_x(1, 512, 576)
-        pw0 = weight_transposes(0, "X0")
-        pw1 = weight_transposes(1, "X1")
-        weight_copy(0, pw0, False)
-        weight_copy(1, pw1, False)
-        weight_quant(0, 256)
         nc.vector.reciprocal(out=sc[:], in_=sc[:])
         nc.vector.tensor_mul(out=sc[:], in0=sc[:], in1=prmt[:, 2:4])
         nc.vector.tensor_sub(out=bi[:], in0=prmt[:, 0:2], in1=prmt[:, 6:8])
         nc.vector.tensor_mul(out=bi[:], in0=bi[:], in1=sc[:])
         nc.vector.tensor_add(out=bi[:], in0=bi[:], in1=prmt[:, 4:6])
-        pw4 = weight_transposes(4, "T0")
-        pw5 = weight_transposes(5, "T1")
-        weight_copy(4, pw4, False)
-        weight_copy(5, pw5, False)
+        pw2 = weight_transposes(2, "A0")
+        weight_copy(2, pw2, False)
+        quant_x(0, 0, 512)
+        quant_x(0, 512, 576)
+        weight_quant(256, 384)
+        regroup(0, 1, 0, 384, True)
+        regroup(0, 1, 384, 576, False)
+        pw3 = weight_transposes(3, "A1")
+        weight_copy(3, pw3, False)
+        quant_x(1, 0, 512)
+        quant_x(1, 512, 576)
+        weight_quant(384, 512)
+        nc.scalar.copy(out=pmat[:], in_=pmem[:])
+        pw0 = weight_transposes(0, "X0")
+        pw1 = weight_transposes(1, "X1")
+        weight_copy(0, pw0, False)
+        weight_copy(1, pw1, False)
 
         state = {}
 
@@ -407,31 +406,37 @@ def tile_afnb_pa_kernel(tc, low_feats, wk, bk, gk, bek, mk, vk, wv, bv, out_0, o
 
         begin(0)
         v_mx(0, 0, "A0")
+        pw4 = weight_transposes(4, "T0")
+        pw5 = weight_transposes(5, "T1")
+        weight_copy(4, pw4, False)
+        weight_copy(5, pw5, False)
         v_mx(0, 1, "A1")
         v_pool(0, 0)
+        weight_quant(0, 256)
+        regroup(1, 0, 192, 384, "gpsimd")
+        regroup(1, 1, 192, 384, "gpsimd")
+        regroup(1, 0, 384, 576, False)
+        regroup(1, 0, 0, 192, True)
         weight_quant(512, 768)
         px_mx(0, 0, 2, "X0")
         px_mx(0, 2, 4, "X1")
-        regroup(1, 0, 192, 384, "gpsimd")
-        regroup(1, 0, 384, 576, False)
+        quant_x(0, 576, 640)
+        quant_x(0, 640, 1152)
         v_pool(0, 1)
-        px_pool(0, 0, 2)
         u_mx(0, 0, "A0")
         px_mx(0, 4, 5, "X0")
-        regroup(1, 1, 192, 384, "gpsimd")
         regroup(1, 1, 384, 576, False)
+        regroup(1, 1, 0, 192, True)
+        px_pool(0, 0, 2)
         px_pool(0, 2, 4)
         u_mx(0, 1, "A1")
         u_pool_gpsimd(0, 0)
         px_pool(0, 4, 5)
-        regroup(1, 0, 0, 192, True)
-        regroup(1, 1, 0, 192, True)
-        u_pool_gpsimd(0, 1)
-        for g in range(2):
-            quant_x(g, 576, 640)
-            quant_x(g, 640, 1152)
         v_pool_tail(0)
         coarse_grids(0, 2)
+        quant_x(1, 576, 640)
+        quant_x(1, 640, 1152)
+        u_pool_gpsimd(0, 1)
 
         begin(1)
         v_mx(1, 0, "A0")
@@ -444,13 +449,13 @@ def tile_afnb_pa_kernel(tc, low_feats, wk, bk, gk, bek, mk, vk, wv, bv, out_0, o
         v_mx(1, 1, "A1")
         u_mx(1, 1, "A0")
         u_pool(1, 0)
-        px_pool(1, 0, 2)
         px_mx(1, 4, 5, "X0")
+        px_pool(1, 0, 2)
         v_pool(1, 1)
+        v_pool_tail(1)
         px_pool(1, 2, 4)
         px_pool(1, 4, 5)
         u_pool(1, 1)
-        v_pool_tail(1)
         coarse_grids(2, 8)
         value_transposes(1)
         finish_keys()

@@ -33,7 +33,6 @@ def tile_afnb_pa_kernel(tc, low_feats, wk, bk, gk, bek, mk, vk, wv, bv, out_0, o
         ctx.enter_context(tc.manual_schedule())
 
         prm = keep.tile([P, P], BF16)
-        bvrow = keep.tile([P, 512], BF16)
         w_sb = keep.tile([P, 6 * 1024], BF16)
         xr = []
         for b in range(NB):
@@ -52,7 +51,6 @@ def tile_afnb_pa_kernel(tc, low_feats, wk, bk, gk, bek, mk, vk, wv, bv, out_0, o
         mflat = member[:].rearrange("p h w -> p (h w)")
         mtail = keep.tile([P, P], BF16)
         pmat = keep.tile([P, 5, P], F32)
-        ones = keep.tile([P, P], BF16)
         wloc = keep.tile([P, NLOC], F32)
         rtmp = keep.tile([P, NLOC], F32)
         rs = keep.tile([P, 1], F32)
@@ -60,7 +58,7 @@ def tile_afnb_pa_kernel(tc, low_feats, wk, bk, gk, bek, mk, vk, wv, bv, out_0, o
         prmt = keep.tile([P, 10], F32)
         sc = keep.tile([P, 2], F32)
         bi = keep.tile([P, 2], F32)
-        bvb = keep.tile([P, 512], F32)
+        bvb = keep.tile([P, 512], BF16)
         wf = w_sb[:].bitcast(F32)
         wg = keep.tile([P, 2 * CH * 4], BF16, align_bytes=64)
         wgf = wg[:].bitcast(F32).rearrange("p (g c u) -> p g c u", g=2, u=2)
@@ -170,14 +168,11 @@ def tile_afnb_pa_kernel(tc, low_feats, wk, bk, gk, bek, mk, vk, wv, bv, out_0, o
             nc.vector.tensor_reduce(out=dst6, in_=src6, axis=AX.XY, op=ALU.add)
 
         nc.vector.memset(prm[:], 0.0)
-        nc.vector.memset(bvrow[:], 0.0)
-        nc.vector.memset(ones[:], 1.0)
         nc.vector.memset(warm[:], 1.0)
         for i, vec in enumerate((bk, gk, bek, mk, vk)):
             nc.scalar.dma_start(
                 out=prm[2 * i : 2 * i + 2, :], in_=vec.rearrange("(r p) -> r p", p=P)
             )
-        nc.scalar.dma_start(out=bvrow[0:1, :], in_=bv.rearrange("(o c) -> o c", o=1))
         load_x(0, 0)
         load_w(2, 1, wv[256:384, :])
         load_x(0, 1)
@@ -186,6 +181,7 @@ def tile_afnb_pa_kernel(tc, low_feats, wk, bk, gk, bek, mk, vk, wv, bv, out_0, o
         load_w(4, 2, wk)
         load_x(1, 0)
         load_x(1, 1)
+        nc.sync.dma_start(out=bvb[:], in_=bv.partition_broadcast(P))
         make_identity(nc, ident_b[:])
         make_identity(nc, ident_f[:])
         nc.scalar.activation(out=warm[:], in_=warm[:], func=ACT.Sqrt)
@@ -210,6 +206,13 @@ def tile_afnb_pa_kernel(tc, low_feats, wk, bk, gk, bek, mk, vk, wv, bv, out_0, o
         nc.vector.tensor_scalar_add(out=mflat, in0=mflat, scalar1=ident_f[:, 0:1])
         nc.vector.memset(mtail[:], 0.0)
         nc.vector.tensor_copy(out=mtail[:, 64:128], in_=mflat[:, 512:576])
+        pmem = psum.tile([P, 5, P], BF16, tag="B0")
+        for m in range(4):
+            nc.tensor.transpose(
+                out=pmem[:, m, :], in_=mflat[:, P * m : P * m + P], identity=ident_b[:]
+            )
+        nc.tensor.transpose(out=pmem[:, 4, :], in_=mtail[:], identity=ident_b[:])
+        nc.scalar.copy(out=pmat[:], in_=pmem[:])
         nc.vector.memset(wloc[:, 0:1], 576.0)
         nc.vector.memset(wloc[:, 1:10], 64.0)
         nc.vector.memset(wloc[:, 10:46], 16.0)
@@ -219,45 +222,29 @@ def tile_afnb_pa_kernel(tc, low_feats, wk, bk, gk, bek, mk, vk, wv, bv, out_0, o
         nc.vector.tensor_reduce(out=rs[:], in_=rtmp[:], axis=AX.X, op=ALU.add)
         nc.vector.memset(sums[:, :, :, NLOC:P], 0.0)
 
-        pbv = psum.tile([P, 512], F32, tag="T1")
-        nc.tensor.matmul(out=pbv[:], lhsT=ones[:], rhs=bvrow[:], start=True, stop=True)
-        pprm = psum.tile([P, P], BF16, tag="B1")
-        nc.tensor.transpose(out=pprm[:], in_=prm[:], identity=ident_b[:])
-        pmem = psum.tile([P, 5, P], BF16, tag="B0")
-        for m in range(4):
-            nc.tensor.transpose(
-                out=pmem[:, m, :], in_=mflat[:, P * m : P * m + P], identity=ident_b[:]
-            )
-        nc.tensor.transpose(out=pmem[:, 4, :], in_=mtail[:], identity=ident_b[:])
-        nc.scalar.copy(out=bvb[:], in_=pbv[:])
-        nc.vector.tensor_copy(out=prmt[:], in_=pprm[:, 0:10])
-        nc.vector.tensor_scalar_add(out=sc[:], in0=prmt[:, 8:10], scalar1=EPS)
-        nc.scalar.activation(out=sc[:], in_=sc[:], func=ACT.Sqrt)
-
         regroup(0, 0, 0, 384, True)
         regroup(0, 0, 384, 576, False)
-        nc.vector.reciprocal(out=sc[:], in_=sc[:])
-        nc.vector.tensor_mul(out=sc[:], in0=sc[:], in1=prmt[:, 2:4])
-        nc.vector.tensor_sub(out=bi[:], in0=prmt[:, 0:2], in1=prmt[:, 6:8])
-        nc.vector.tensor_mul(out=bi[:], in0=bi[:], in1=sc[:])
-        nc.vector.tensor_add(out=bi[:], in0=bi[:], in1=prmt[:, 4:6])
         pw2 = weight_transposes(2, "A0")
         weight_copy(2, pw2, False)
         quant_x(0, 0, 512)
         quant_x(0, 512, 576)
-        weight_quant(256, 384)
+        pprm = psum.tile([P, P], BF16, tag="B1")
+        nc.tensor.transpose(out=pprm[:], in_=prm[:], identity=ident_b[:])
         regroup(0, 1, 0, 384, True)
         regroup(0, 1, 384, 576, False)
+        weight_quant(256, 384)
+        nc.vector.tensor_copy(out=prmt[:], in_=pprm[:, 0:10])
+        nc.vector.tensor_scalar_add(out=sc[:], in0=prmt[:, 8:10], scalar1=EPS)
         pw3 = weight_transposes(3, "A1")
         weight_copy(3, pw3, False)
+        nc.scalar.activation(out=sc[:], in_=sc[:], func=ACT.Sqrt)
         quant_x(1, 0, 512)
         quant_x(1, 512, 576)
-        weight_quant(384, 512)
-        nc.scalar.copy(out=pmat[:], in_=pmem[:])
         pw0 = weight_transposes(0, "X0")
         pw1 = weight_transposes(1, "X1")
         weight_copy(0, pw0, False)
         weight_copy(1, pw1, False)
+        weight_quant(384, 512)
 
         state = {}
 
@@ -406,36 +393,39 @@ def tile_afnb_pa_kernel(tc, low_feats, wk, bk, gk, bek, mk, vk, wv, bv, out_0, o
 
         begin(0)
         v_mx(0, 0, "A0")
+        nc.vector.reciprocal(out=sc[:], in_=sc[:])
+        nc.vector.tensor_mul(out=sc[:], in0=sc[:], in1=prmt[:, 2:4])
+        nc.vector.tensor_sub(out=bi[:], in0=prmt[:, 0:2], in1=prmt[:, 6:8])
+        nc.vector.tensor_mul(out=bi[:], in0=bi[:], in1=sc[:])
+        nc.vector.tensor_add(out=bi[:], in0=bi[:], in1=prmt[:, 4:6])
         pw4 = weight_transposes(4, "T0")
         pw5 = weight_transposes(5, "T1")
         weight_copy(4, pw4, False)
         weight_copy(5, pw5, False)
         v_mx(0, 1, "A1")
-        v_pool(0, 0)
         weight_quant(0, 256)
-        regroup(1, 0, 192, 384, "gpsimd")
-        regroup(1, 1, 192, 384, "gpsimd")
-        regroup(1, 0, 384, 576, False)
-        regroup(1, 0, 0, 192, True)
-        weight_quant(512, 768)
+        v_pool(0, 0)
+        regroup(1, 0, 288, 576, "gpsimd")
+        regroup(1, 1, 288, 576, "gpsimd")
         px_mx(0, 0, 2, "X0")
         px_mx(0, 2, 4, "X1")
-        quant_x(0, 576, 640)
-        quant_x(0, 640, 1152)
+        weight_quant(512, 768)
+        regroup(1, 0, 0, 288, True)
         v_pool(0, 1)
         u_mx(0, 0, "A0")
         px_mx(0, 4, 5, "X0")
-        regroup(1, 1, 384, 576, False)
-        regroup(1, 1, 0, 192, True)
+        quant_x(0, 576, 640)
+        quant_x(0, 640, 1152)
+        regroup(1, 1, 0, 288, True)
         px_pool(0, 0, 2)
-        px_pool(0, 2, 4)
         u_mx(0, 1, "A1")
+        px_pool(0, 2, 4)
         u_pool_gpsimd(0, 0)
+        quant_x(1, 576, 640)
+        quant_x(1, 640, 1152)
         px_pool(0, 4, 5)
         v_pool_tail(0)
         coarse_grids(0, 2)
-        quant_x(1, 576, 640)
-        quant_x(1, 640, 1152)
         u_pool_gpsimd(0, 1)
 
         begin(1)
@@ -452,10 +442,10 @@ def tile_afnb_pa_kernel(tc, low_feats, wk, bk, gk, bek, mk, vk, wv, bv, out_0, o
         px_mx(1, 4, 5, "X0")
         px_pool(1, 0, 2)
         v_pool(1, 1)
-        v_pool_tail(1)
         px_pool(1, 2, 4)
         px_pool(1, 4, 5)
         u_pool(1, 1)
+        v_pool_tail(1)
         coarse_grids(2, 8)
         value_transposes(1)
         finish_keys()

@@ -33,6 +33,7 @@ def tile_afnb_pa_kernel(tc, low_feats, wk, bk, gk, bek, mk, vk, wv, bv, out_0, o
         ctx.enter_context(tc.manual_schedule())
 
         prm = keep.tile([P, P], BF16)
+        bvrow = keep.tile([P, 512], BF16)
         w_sb = keep.tile([P, 6 * 1024], BF16)
         xr = []
         for b in range(NB):
@@ -51,6 +52,7 @@ def tile_afnb_pa_kernel(tc, low_feats, wk, bk, gk, bek, mk, vk, wv, bv, out_0, o
         mflat = member[:].rearrange("p h w -> p (h w)")
         mtail = keep.tile([P, P], BF16)
         pmat = keep.tile([P, 5, P], F32)
+        ones = keep.tile([P, P], BF16)
         wloc = keep.tile([P, NLOC], F32)
         rtmp = keep.tile([P, NLOC], F32)
         rs = keep.tile([P, 1], F32)
@@ -58,7 +60,7 @@ def tile_afnb_pa_kernel(tc, low_feats, wk, bk, gk, bek, mk, vk, wv, bv, out_0, o
         prmt = keep.tile([P, 10], F32)
         sc = keep.tile([P, 2], F32)
         bi = keep.tile([P, 2], F32)
-        bvb = keep.tile([P, 512], BF16)
+        bvb = keep.tile([P, 512], F32)
         wf = w_sb[:].bitcast(F32)
         wg = keep.tile([P, 2 * CH * 4], BF16, align_bytes=64)
         wgf = wg[:].bitcast(F32).rearrange("p (g c u) -> p g c u", g=2, u=2)
@@ -168,11 +170,14 @@ def tile_afnb_pa_kernel(tc, low_feats, wk, bk, gk, bek, mk, vk, wv, bv, out_0, o
             nc.vector.tensor_reduce(out=dst6, in_=src6, axis=AX.XY, op=ALU.add)
 
         nc.vector.memset(prm[:], 0.0)
+        nc.vector.memset(bvrow[:], 0.0)
+        nc.vector.memset(ones[:], 1.0)
         nc.vector.memset(warm[:], 1.0)
         for i, vec in enumerate((bk, gk, bek, mk, vk)):
             nc.scalar.dma_start(
                 out=prm[2 * i : 2 * i + 2, :], in_=vec.rearrange("(r p) -> r p", p=P)
             )
+        nc.scalar.dma_start(out=bvrow[0:1, :], in_=bv.rearrange("(o c) -> o c", o=1))
         load_x(0, 0)
         load_w(2, 1, wv[256:384, :])
         load_x(0, 1)
@@ -181,7 +186,6 @@ def tile_afnb_pa_kernel(tc, low_feats, wk, bk, gk, bek, mk, vk, wv, bv, out_0, o
         load_w(4, 2, wk)
         load_x(1, 0)
         load_x(1, 1)
-        nc.sync.dma_start(out=bvb[:], in_=bv.partition_broadcast(P))
         make_identity(nc, ident_b[:])
         make_identity(nc, ident_f[:])
         nc.scalar.activation(out=warm[:], in_=warm[:], func=ACT.Sqrt)
@@ -206,13 +210,6 @@ def tile_afnb_pa_kernel(tc, low_feats, wk, bk, gk, bek, mk, vk, wv, bv, out_0, o
         nc.vector.tensor_scalar_add(out=mflat, in0=mflat, scalar1=ident_f[:, 0:1])
         nc.vector.memset(mtail[:], 0.0)
         nc.vector.tensor_copy(out=mtail[:, 64:128], in_=mflat[:, 512:576])
-        pmem = psum.tile([P, 5, P], BF16, tag="B0")
-        for m in range(4):
-            nc.tensor.transpose(
-                out=pmem[:, m, :], in_=mflat[:, P * m : P * m + P], identity=ident_b[:]
-            )
-        nc.tensor.transpose(out=pmem[:, 4, :], in_=mtail[:], identity=ident_b[:])
-        nc.scalar.copy(out=pmat[:], in_=pmem[:])
         nc.vector.memset(wloc[:, 0:1], 576.0)
         nc.vector.memset(wloc[:, 1:10], 64.0)
         nc.vector.memset(wloc[:, 10:46], 16.0)
@@ -222,29 +219,45 @@ def tile_afnb_pa_kernel(tc, low_feats, wk, bk, gk, bek, mk, vk, wv, bv, out_0, o
         nc.vector.tensor_reduce(out=rs[:], in_=rtmp[:], axis=AX.X, op=ALU.add)
         nc.vector.memset(sums[:, :, :, NLOC:P], 0.0)
 
+        pbv = psum.tile([P, 512], F32, tag="T1")
+        nc.tensor.matmul(out=pbv[:], lhsT=ones[:], rhs=bvrow[:], start=True, stop=True)
+        pprm = psum.tile([P, P], BF16, tag="B1")
+        nc.tensor.transpose(out=pprm[:], in_=prm[:], identity=ident_b[:])
+        pmem = psum.tile([P, 5, P], BF16, tag="B0")
+        for m in range(4):
+            nc.tensor.transpose(
+                out=pmem[:, m, :], in_=mflat[:, P * m : P * m + P], identity=ident_b[:]
+            )
+        nc.tensor.transpose(out=pmem[:, 4, :], in_=mtail[:], identity=ident_b[:])
+        nc.scalar.copy(out=bvb[:], in_=pbv[:])
+        nc.vector.tensor_copy(out=prmt[:], in_=pprm[:, 0:10])
+        nc.vector.tensor_scalar_add(out=sc[:], in0=prmt[:, 8:10], scalar1=EPS)
+        nc.scalar.activation(out=sc[:], in_=sc[:], func=ACT.Sqrt)
+
         regroup(0, 0, 0, 384, True)
         regroup(0, 0, 384, 576, False)
+        nc.vector.reciprocal(out=sc[:], in_=sc[:])
+        nc.vector.tensor_mul(out=sc[:], in0=sc[:], in1=prmt[:, 2:4])
+        nc.vector.tensor_sub(out=bi[:], in0=prmt[:, 0:2], in1=prmt[:, 6:8])
+        nc.vector.tensor_mul(out=bi[:], in0=bi[:], in1=sc[:])
+        nc.vector.tensor_add(out=bi[:], in0=bi[:], in1=prmt[:, 4:6])
         pw2 = weight_transposes(2, "A0")
         weight_copy(2, pw2, False)
         quant_x(0, 0, 512)
         quant_x(0, 512, 576)
-        pprm = psum.tile([P, P], BF16, tag="B1")
-        nc.tensor.transpose(out=pprm[:], in_=prm[:], identity=ident_b[:])
+        weight_quant(256, 384)
         regroup(0, 1, 0, 384, True)
         regroup(0, 1, 384, 576, False)
-        weight_quant(256, 384)
-        nc.vector.tensor_copy(out=prmt[:], in_=pprm[:, 0:10])
-        nc.vector.tensor_scalar_add(out=sc[:], in0=prmt[:, 8:10], scalar1=EPS)
         pw3 = weight_transposes(3, "A1")
         weight_copy(3, pw3, False)
-        nc.scalar.activation(out=sc[:], in_=sc[:], func=ACT.Sqrt)
         quant_x(1, 0, 512)
         quant_x(1, 512, 576)
+        weight_quant(384, 512)
+        nc.scalar.copy(out=pmat[:], in_=pmem[:])
         pw0 = weight_transposes(0, "X0")
         pw1 = weight_transposes(1, "X1")
         weight_copy(0, pw0, False)
         weight_copy(1, pw1, False)
-        weight_quant(384, 512)
 
         state = {}
 
@@ -393,39 +406,34 @@ def tile_afnb_pa_kernel(tc, low_feats, wk, bk, gk, bek, mk, vk, wv, bv, out_0, o
 
         begin(0)
         v_mx(0, 0, "A0")
-        nc.vector.reciprocal(out=sc[:], in_=sc[:])
-        nc.vector.tensor_mul(out=sc[:], in0=sc[:], in1=prmt[:, 2:4])
-        nc.vector.tensor_sub(out=bi[:], in0=prmt[:, 0:2], in1=prmt[:, 6:8])
-        nc.vector.tensor_mul(out=bi[:], in0=bi[:], in1=sc[:])
-        nc.vector.tensor_add(out=bi[:], in0=bi[:], in1=prmt[:, 4:6])
         pw4 = weight_transposes(4, "T0")
         pw5 = weight_transposes(5, "T1")
         weight_copy(4, pw4, False)
         weight_copy(5, pw5, False)
         v_mx(0, 1, "A1")
-        weight_quant(0, 256)
         v_pool(0, 0)
-        regroup(1, 0, 288, 576, "gpsimd")
-        regroup(1, 1, 288, 576, "gpsimd")
+        weight_quant(0, 256)
+        regroup(1, 0, 384, 576, False)
+        regroup(1, 0, 0, 384, True)
+        weight_quant(512, 768)
         px_mx(0, 0, 2, "X0")
         px_mx(0, 2, 4, "X1")
-        weight_quant(512, 768)
-        regroup(1, 0, 0, 288, True)
+        quant_x(0, 576, 640)
+        quant_x(0, 640, 1152)
         v_pool(0, 1)
         u_mx(0, 0, "A0")
         px_mx(0, 4, 5, "X0")
-        quant_x(0, 576, 640)
-        quant_x(0, 640, 1152)
-        regroup(1, 1, 0, 288, True)
+        regroup(1, 1, 384, 576, False)
+        regroup(1, 1, 0, 384, True)
         px_pool(0, 0, 2)
-        u_mx(0, 1, "A1")
         px_pool(0, 2, 4)
+        u_mx(0, 1, "A1")
         u_pool_gpsimd(0, 0)
-        quant_x(1, 576, 640)
-        quant_x(1, 640, 1152)
         px_pool(0, 4, 5)
         v_pool_tail(0)
         coarse_grids(0, 2)
+        quant_x(1, 576, 640)
+        quant_x(1, 640, 1152)
         u_pool_gpsimd(0, 1)
 
         begin(1)
@@ -442,10 +450,10 @@ def tile_afnb_pa_kernel(tc, low_feats, wk, bk, gk, bek, mk, vk, wv, bv, out_0, o
         px_mx(1, 4, 5, "X0")
         px_pool(1, 0, 2)
         v_pool(1, 1)
+        v_pool_tail(1)
         px_pool(1, 2, 4)
         px_pool(1, 4, 5)
         u_pool(1, 1)
-        v_pool_tail(1)
         coarse_grids(2, 8)
         value_transposes(1)
         finish_keys()

from contextlib import ExitStack

import concourse.mybir as mybir
from concourse.masks import make_identity

F32 = mybir.dt.float32
BF16 = mybir.dt.bfloat16
U32 = mybir.dt.uint32
U8 = mybir.dt.uint8
FP8X4 = mybir.dt.float8_e4m3fn_x4
ALU = mybir.AluOpType
ACT = mybir.ActivationFunctionType
AX = mybir.AxisListType

P = 128
NB = 2
NPX = 576
NX = NB * NPX
CH = 768
NLOC = 110
EPS = 1e-5
FLOPS = 2 * 768 * 1024 * 1152
PX_STARTS = (0, 128, 256, 384, 448)


def tile_afnb_pa_kernel(tc, low_feats, wk, bk, gk, bek, mk, vk, wv, bv, out_0, out_1):
    nc = tc.nc
    with ExitStack() as ctx:
        keep = ctx.enter_context(tc.tile_pool(name="keep", bufs=1))
        work = ctx.enter_context(tc.tile_pool(name="work", bufs=2))
        vpool = ctx.enter_context(tc.tile_pool(name="vpool", bufs=3))
        psum = ctx.enter_context(tc.psum_pool(name="psum", bufs=1))
        ctx.enter_context(tc.manual_schedule())

        prm = keep.tile([P, P], BF16)
        bvrow = keep.tile([P, 512], BF16)
        w_sb = keep.tile([P, 6 * 1024], BF16)
        xr = []
        for b in range(NB):
            row = []
            for g in range(2):
                xr_bg = keep.tile([P, 4, NPX], BF16, name="xr%d%d" % (b, g))
                row.append(xr_bg)
            xr.append(row)
        ident_b = keep.tile([P, P], BF16)
        ident_f = keep.tile([P, P], F32)
        warm = keep.tile([P, 1], F32)
        q8 = keep.tile([P, 8, 24], BF16)
        q6 = keep.tile([P, 6, 24], BF16)
        q3 = keep.tile([P, 3, 24], BF16)
        member = keep.tile([P, 24, 24], BF16)
        mflat = member[:].rearrange("p h w -> p (h w)")
        mtail = keep.tile([P, P], BF16)
        pmat = keep.tile([P, 5, P], F32)
        ones = keep.tile([P, P], BF16)
        wloc = keep.tile([P, NLOC], F32)
        rtmp = keep.tile([P, NLOC], F32)
        rs = keep.tile([P, 1], F32)
        sums = keep.tile([P, NB, 4, P], F32)
        prmt = keep.tile([P, 10], F32)
        sc = keep.tile([P, 2], F32)
        bi = keep.tile([P, 2], F32)
        bvb = keep.tile([P, 512], F32)
        wf = w_sb[:].bitcast(F32)
        wg = keep.tile([P, 2 * CH * 4], BF16, align_bytes=64)
        wgf = wg[:].bitcast(F32).rearrange("p (g c u) -> p g c u", g=2, u=2)
        wc = keep.tile([P, 2 * CH], U32, align_bytes=64)
        wsc = keep.tile([P, 2 * CH], U8, align_bytes=64)
        xg = keep.tile([P, 2 * NX * 4], BF16, align_bytes=64)
        xc = keep.tile([P, 2 * NX], U32, align_bytes=64)
        xs = keep.tile([P, 2 * NX], U8, align_bytes=64)

        def load_x(b, g):
            nc.sync.dma_start(
                out=xr[b][g][:].rearrange("p (u e) n -> p u e n", e=2),
                in_=low_feats[b, 512 * g : 512 * g + 512].rearrange(
                    "(u q e) h w -> q u e (h w)", u=2, e=2
                ),
            )

        def load_w(r0, n_blocks, rows):
            nc.sync.dma_start(
                out=w_sb[:, 1024 * r0 : 1024 * (r0 + n_blocks)].rearrange(
                    "p (r k) -> p r k", k=1024
                ),
                in_=rows.rearrange("(r p) k -> p r k", p=P),
            )

        def weight_transposes(r, bank):
            pw = psum.tile([P, 2, 2, P], F32, tag=bank, name="pw%d" % r)
            for g in range(2):
                for u in range(2):
                    c0 = 512 * r + 256 * g + 128 * u
                    nc.tensor.transpose(
                        out=pw[:, g, u, :], in_=wf[:, c0 : c0 + P], identity=ident_f[:]
                    )
            return pw

        def weight_copy(r, pw, on_vector):
            dst = wgf[:, :, P * r : P * r + P, :]
            src = pw[:].rearrange("p g u c -> p g c u")
            if on_vector:
                nc.vector.tensor_copy(out=dst, in_=src)
            else:
                nc.scalar.copy(out=dst, in_=src)

        def weight_quant(c0, c1):
            for g in range(2):
                lo = g * CH + c0
                hi = g * CH + c1
                nc.vector.quantize_mx(
                    out=wc[:, lo:hi].bitcast(FP8X4),
                    scales=wsc[:, lo:hi],
                    in_=wg[:, 4 * lo : 4 * hi],
                )

        def regroup(b, g, a0, a1, on_vector):
            base = g * NX + NPX * b
            dst = xg[:, 4 * (base + a0) : 4 * (base + a1)].rearrange(
                "p (c i t) -> p c t i", i=4, t=4
            )
            src = xr[b][g][:, :, a0:a1].rearrange("p t (c i) -> p c t i", i=4)
            if on_vector == "gpsimd":
                nc.gpsimd.tensor_scalar(
                    out=dst, in0=src, scalar1=1.0, scalar2=0.0, op0=ALU.mult, op1=ALU.add
                )
            elif on_vector:
                nc.vector.tensor_copy(out=dst, in_=src)
            else:
                nc.scalar.copy(out=dst, in_=src)

        def quant_x(g, lo, hi):
            lo = g * NX + lo
            hi = g * NX + hi
            nc.vector.quantize_mx(
                out=xc[:, lo:hi].bitcast(FP8X4),
                scales=xs[:, lo:hi],
                in_=xg[:, 4 * lo : 4 * hi],
            )

        def mx_group(out, blk, lo, n):
            for g in range(2):
                w0 = g * CH + P * blk
                x0 = g * NX + lo
                nc.tensor.matmul_mx(
                    out=out,
                    lhsT=wc[:, w0 : w0 + P].bitcast(FP8X4),
                    lhsT_scale=wsc[:, w0 : w0 + P],
                    rhs=xc[:, x0 : x0 + n].bitcast(FP8X4),
                    rhs_scale=xs[:, x0 : x0 + n],
                    start=(g == 0),
                    stop=(g == 1),
                )

        def px_group(out, lo):
            for g in range(2):
                x0 = g * NX + lo
                nc.tensor.matmul_mx(
                    out=out,
                    lhsT=xc[:, x0 : x0 + P].bitcast(FP8X4),
                    lhsT_scale=xs[:, x0 : x0 + P],
                    rhs=wc[:, g * CH : g * CH + 256].bitcast(FP8X4),
                    rhs_scale=wsc[:, g * CH : g * CH + 256],
                    start=(g == 0),
                    stop=(g == 1),
                )

        def pool_pair(src8, dst8, src6, dst6):
            nc.vector.tensor_reduce(out=dst8, in_=src8, axis=AX.XY, op=ALU.add)
            nc.vector.tensor_reduce(out=dst6, in_=src6, axis=AX.XY, op=ALU.add)

        nc.vector.memset(prm[:], 0.0)
        nc.vector.memset(bvrow[:], 0.0)
        nc.vector.memset(ones[:], 1.0)
        nc.vector.memset(warm[:], 1.0)
        for i, vec in enumerate((bk, gk, bek, mk, vk)):
            nc.scalar.dma_start(
                out=prm[2 * i : 2 * i + 2, :], in_=vec.rearrange("(r p) -> r p", p=P)
            )
        nc.scalar.dma_start(out=bvrow[0:1, :], in_=bv.rearrange("(o c) -> o c", o=1))
        load_x(0, 0)
        load_w(2, 1, wv[256:384, :])
        load_x(0, 1)
        load_w(3, 1, wv[384:512, :])
        load_w(0, 2, wv[0:256, :])
        load_w(4, 2, wk)
        load_x(1, 0)
        load_x(1, 1)
        make_identity(nc, ident_b[:])
        make_identity(nc, ident_f[:])
        nc.scalar.activation(out=warm[:], in_=warm[:], func=ACT.Sqrt)

        for qt, off, grid, bs in ((q8, 46, 8, 3), (q6, 10, 6, 4), (q3, 1, 3, 8)):
            nc.vector.tensor_copy(
                out=qt[:].rearrange("p g (c j) -> p g c j", j=bs),
                in_=ident_b[:, off : off + grid * grid]
                .rearrange("p (g c) -> p g c", c=grid)
                .unsqueeze(3)
                .to_broadcast([P, grid, grid, bs]),
            )
        nc.vector.tensor_copy(
            out=member[:].rearrange("p (g i) w -> p g i w", i=3),
            in_=q8[:].unsqueeze(2).to_broadcast([P, 8, 3, 24]),
        )
        for qt, grid, bs in ((q6, 6, 4), (q3, 3, 8)):
            mv = member[:].rearrange("p (g i) w -> p g i w", i=bs)
            nc.vector.tensor_tensor(
                out=mv, in0=mv, in1=qt[:].unsqueeze(2).to_broadcast([P, grid, bs, 24]), op=ALU.add
            )
        nc.vector.tensor_scalar_add(out=mflat, in0=mflat, scalar1=ident_f[:, 0:1])
        nc.vector.memset(mtail[:], 0.0)
        nc.vector.tensor_copy(out=mtail[:, 64:128], in_=mflat[:, 512:576])
        nc.vector.memset(wloc[:, 0:1], 576.0)
        nc.vector.memset(wloc[:, 1:10], 64.0)
        nc.vector.memset(wloc[:, 10:46], 16.0)
        nc.vector.memset(wloc[:, 46:110], 9.0)
        nc.vector.reciprocal(out=wloc[:], in_=wloc[:])
        nc.vector.tensor_mul(out=rtmp[:], in0=ident_f[:, 0:NLOC], in1=wloc[:])
        nc.vector.tensor_reduce(out=rs[:], in_=rtmp[:], axis=AX.X, op=ALU.add)
        nc.vector.memset(sums[:, :, :, NLOC:P], 0.0)

        pbv = psum.tile([P, 512], F32, tag="T1")
        nc.tensor.matmul(out=pbv[:], lhsT=ones[:], rhs=bvrow[:], start=True, stop=True)
        pprm = psum.tile([P, P], BF16, tag="B1")
        nc.tensor.transpose(out=pprm[:], in_=prm[:], identity=ident_b[:])
        pmem = psum.tile([P, 5, P], BF16, tag="B0")
        for m in range(4):
            nc.tensor.transpose(
                out=pmem[:, m, :], in_=mflat[:, P * m : P * m + P], identity=ident_b[:]
            )
        nc.tensor.transpose(out=pmem[:, 4, :], in_=mtail[:], identity=ident_b[:])
        nc.scalar.copy(out=bvb[:], in_=pbv[:])
        nc.vector.tensor_copy(out=prmt[:], in_=pprm[:, 0:10])
        nc.vector.tensor_scalar_add(out=sc[:], in0=prmt[:, 8:10], scalar1=EPS)
        nc.scalar.activation(out=sc[:], in_=sc[:], func=ACT.Sqrt)

        regroup(0, 0, 0, 384, True)
        regroup(0, 0, 384, 576, False)
        nc.vector.reciprocal(out=sc[:], in_=sc[:])
        nc.vector.tensor_mul(out=sc[:], in0=sc[:], in1=prmt[:, 2:4])
        nc.vector.tensor_sub(out=bi[:], in0=prmt[:, 0:2], in1=prmt[:, 6:8])
        nc.vector.tensor_mul(out=bi[:], in0=bi[:], in1=sc[:])
        nc.vector.tensor_add(out=bi[:], in0=bi[:], in1=prmt[:, 4:6])
        pw2 = weight_transposes(2, "A0")
        weight_copy(2, pw2, False)
        quant_x(0, 0, 512)
        quant_x(0, 512, 576)
        weight_quant(256, 384)
        regroup(0, 1, 0, 384, True)
        regroup(0, 1, 384, 576, False)
        pw3 = weight_transposes(3, "A1")
        weight_copy(3, pw3, False)
        quant_x(1, 0, 512)
        quant_x(1, 512, 576)
        weight_quant(384, 512)
        nc.scalar.copy(out=pmat[:], in_=pmem[:])
        pw0 = weight_transposes(0, "X0")
        pw1 = weight_transposes(1, "X1")
        weight_copy(0, pw0, False)
        weight_copy(1, pw1, False)

        state = {}

        def begin(b):
            state["pt", b] = psum.tile([P, 512], F32, tag="T%d" % b, name="pt%d" % b)
            state["pbv", b] = psum.tile([P, 2, P], F32, tag="B0", name="pb_v%d" % b)
            state["pbu", b] = psum.tile([P, 2, P], F32, tag="B1", name="pb_u%d" % b)
            state["r", b] = work.tile([P, 2, NPX], F32, tag="r_sb", name="r_sb%d" % b)

        def v_mx(b, k, bank):
            pa = psum.tile([P, 512], F32, tag=bank, name="pav%d%d" % (b, k))
            mx_group(pa[:], 2 + k, NPX * b, 512)
            mx_group(state["pbv", b][:, k, :], 2 + k, NPX * b + 448, P)
            state["pav", b, k] = pa

        def v_pool(b, k):
            pa = state["pav", b, k]
            pool_pair(
                pa[:, 0:504].rearrange("p (g i c j) -> p g c i j", i=3, c=8, j=3),
                sums[:, b, k, 46:102].rearrange("p (g c) -> p g c", c=8),
                pa[:, 0:480].rearrange("p (g i c j) -> p g c i j", i=4, c=6, j=4),
                sums[:, b, k, 10:40].rearrange("p (g c) -> p g c", c=6),
            )

        def v_pool_tail(b):
            pb_v = state["pbv", b]
            pool_pair(
                pb_v[:, :, 56:128].rearrange("p k (i c j) -> p k c i j", i=3, c=8, j=3),
                sums[:, b, 0:2, 102:110],
                pb_v[:, :, 32:128].rearrange("p k (i c j) -> p k c i j", i=4, c=6, j=4),
                sums[:, b, 0:2, 40:46],
            )

        def u_mx(b, k, bank):
            pa = psum.tile([P, 512], F32, tag=bank, name="pau%d%d" % (b, k))
            mx_group(pa[:], 4 + k, NPX * b, 512)
            mx_group(state["pbu", b][:, k, :], 4 + k, NPX * b + 448, P)
            r_sb = state["r", b]
            nc.scalar.activation(
                out=r_sb[:, k, 0:512], in_=pa[:], func=ACT.Relu,
                bias=bi[:, k : k + 1], scale=sc[:, k : k + 1],
            )
            nc.scalar.activation(
                out=r_sb[:, k, 512:576], in_=state["pbu", b][:, k, 64:128], func=ACT.Relu,
                bias=bi[:, k : k + 1], scale=sc[:, k : k + 1],
            )

        def u_pool(b, k):
            r_sb = state["r", b]
            pool_pair(
                r_sb[:, k, :].rearrange("p (g i c j) -> p g c i j", i=3, c=8, j=3),
                sums[:, b, 2 + k, 46:110].rearrange("p (g c) -> p g c", c=8),
                r_sb[:, k, :].rearrange("p (g i c j) -> p g c i j", i=4, c=6, j=4),
                sums[:, b, 2 + k, 10:46].rearrange("p (g c) -> p g c", c=6),
            )

        def u_pool_gpsimd(b, k):
            r_k = state["r", b][:, k, :]
            add = ALU.add
            tg = "%d%d" % (b, k)
            rv3 = r_k.rearrange("p (m j) -> p m j", j=3)
            t8 = work.tile([P, 192], F32, tag="t8", name="t8_" + tg)
            nc.gpsimd.tensor_tensor(out=t8[:], in0=rv3[:, :, 0], in1=rv3[:, :, 1], op=add)
            nc.gpsimd.tensor_tensor(out=t8[:], in0=t8[:], in1=rv3[:, :, 2], op=add)
            t8v = t8[:].rearrange("p (g i c) -> p g i c", i=3, c=8)
            u8 = work.tile([P, 8, 8], F32, tag="u8", name="u8_" + tg)
            nc.gpsimd.tensor_tensor(out=u8[:], in0=t8v[:, :, 0, :], in1=t8v[:, :, 1, :], op=add)
            nc.gpsimd.tensor_tensor(
                out=sums[:, b, 2 + k, 46:110].rearrange("p (g c) -> p g c", c=8),
                in0=u8[:], in1=t8v[:, :, 2, :], op=add,
            )
            rv2 = r_k.rearrange("p (m j) -> p m j", j=2)
            p6 = work.tile([P, 288], F32, tag="p6", name="p6_" + tg)
            nc.gpsimd.tensor_tensor(out=p6[:], in0=rv2[:, :, 0], in1=rv2[:, :, 1], op=add)
            p6v = p6[:].rearrange("p (m j) -> p m j", j=2)
            p6b = work.tile([P, 144], F32, tag="p6b", name="p6b_" + tg)
            nc.gpsimd.tensor_tensor(out=p6b[:], in0=p6v[:, :, 0], in1=p6v[:, :, 1], op=add)
            p6bv = p6b[:].rearrange("p (a e c) -> p a e c", e=2, c=6)
            h6 = work.tile([P, 12, 6], F32, tag="h6", name="h6_" + tg)
            nc.gpsimd.tensor_tensor(out=h6[:], in0=p6bv[:, :, 0, :], in1=p6bv[:, :, 1, :], op=add)
            h6v = h6[:].rearrange("p (g a) c -> p g a c", a=2)
            nc.gpsimd.tensor_tensor(
                out=sums[:, b, 2 + k, 10:46].rearrange("p (g c) -> p g c", c=6),
                in0=h6v[:, :, 0, :], in1=h6v[:, :, 1, :], op=add,
            )

        def px_mx(b, m0, m1, bank):
            px = psum.tile([P, 2, 256], F32, tag=bank, name="px%d%d" % (b, m0))
            for m in range(m0, m1):
                px_group(px[:, m - m0, :], NPX * b + PX_STARTS[m])
            vsb = vpool.tile([P, 2, 256], F32, tag="vsb", name="vsb%d%d" % (b, m0))
            nc.scalar.copy(out=vsb[:, 0 : m1 - m0, :], in_=px[:, 0 : m1 - m0, :])
            state["vsb", b, m0] = vsb

        def px_pool(b, m0, m1):
            vsb = state["vsb", b, m0]
            for m in range(m0, m1):
                nc.tensor.matmul(
                    out=state["pt", b][:, 0:256], lhsT=pmat[:, m, :], rhs=vsb[:, m - m0, :],
                    start=(m == 0), stop=(m == 4),
                )

        rows = sums[:].rearrange("p b q l -> p (b q) l")

        def coarse_grids(q0, q1):
            half = work.tile([P, q1 - q0, 18], F32, tag="half%d" % q0, name="half%d" % q0)
            nc.vector.tensor_reduce(
                out=half[:],
                in_=rows[:, q0:q1, 10:46].rearrange("p k (m j) -> p k m j", j=2),
                axis=AX.X, op=ALU.add,
            )
            nc.vector.tensor_reduce(
                out=rows[:, q0:q1, 1:10].rearrange("p k (g c) -> p k g c", c=3),
                in_=half[:].rearrange("p k (g i c) -> p k g c i", i=2, c=3),
                axis=AX.X, op=ALU.add,
            )
            nc.vector.tensor_reduce(
                out=rows[:, q0:q1, 0:1], in_=rows[:, q0:q1, 1:10], axis=AX.X, op=ALU.add
            )

        def value_transposes(b):
            for k in range(2):
                nc.tensor.transpose(
                    out=state["pt", b][:, 256 + P * k : 384 + P * k], in_=sums[:, b, k, :],
                    identity=ident_f[:],
                )

        def finish_value(b):
            vo = work.tile([P, 512], F32, tag="vo", name="vo%d" % b)
            nc.vector.scalar_tensor_tensor(
                out=vo[:], in0=state["pt", b][:], scalar=rs[:, 0:1],
                in1=bvb[:], op0=ALU.mult, op1=ALU.add,
            )
            nc.sync.dma_start(out=out_0[b], in_=vo[0:NLOC, :])

        def finish_keys():
            ko = keep.tile([P, NB, 2, NLOC], F32)
            nc.gpsimd.tensor_tensor(
                out=ko[:], in0=sums[:, :, 2:4, 0:NLOC],
                in1=wloc[:].unsqueeze(1).unsqueeze(1).to_broadcast([P, NB, 2, NLOC]), op=ALU.mult,
            )
            for b in range(NB):
                nc.sync.dma_start(
                    out=out_1[b].rearrange("(k p) l -> p k l", p=P), in_=ko[:, b, :, :]
                )

        begin(0)
        v_mx(0, 0, "A0")
        pw4 = weight_transposes(4, "T0")
        pw5 = weight_transposes(5, "T1")
        weight_copy(4, pw4, False)
        weight_copy(5, pw5, False)
        v_mx(0, 1, "A1")
        v_pool(0, 0)
        weight_quant(0, 256)
        regroup(1, 0, 384, 576, False)
        regroup(1, 0, 0, 384, True)
        weight_quant(512, 768)
        px_mx(0, 0, 2, "X0")
        px_mx(0, 2, 4, "X1")
        quant_x(0, 576, 640)
        quant_x(0, 640, 1152)
        v_pool(0, 1)
        u_mx(0, 0, "A0")
        px_mx(0, 4, 5, "X0")
        regroup(1, 1, 384, 576, False)
        regroup(1, 1, 0, 384, True)
        px_pool(0, 0, 2)
        px_pool(0, 2, 4)
        u_mx(0, 1, "A1")
        u_pool_gpsimd(0, 0)
        px_pool(0, 4, 5)
        v_pool_tail(0)
        coarse_grids(0, 2)
        quant_x(1, 576, 640)
        quant_x(1, 640, 1152)
        u_pool_gpsimd(0, 1)

        begin(1)
        v_mx(1, 0, "A0")
        u_mx(1, 0, "A1")
        value_transposes(0)
        v_pool(1, 0)
        finish_value(0)
        px_mx(1, 0, 2, "X0")
        px_mx(1, 2, 4, "X1")
        v_mx(1, 1, "A1")
        u_mx(1, 1, "A0")
        u_pool(1, 0)
        px_mx(1, 4, 5, "X0")
        px_pool(1, 0, 2)
        v_pool(1, 1)
        v_pool_tail(1)
        px_pool(1, 2, 4)
        px_pool(1, 4, 5)
        u_pool(1, 1)
        coarse_grids(2, 8)
        value_transposes(1)
        finish_keys()
        finish_value(1)
